import numpy as np
import ml_dtypes


def mxq(x, axis, fmt="e4m3"):
    dtype, down = {"e4m3": (ml_dtypes.float8_e4m3fn, 7), "e5m2": (ml_dtypes.float8_e5m2, 14)}[fmt]
    v = np.moveaxis(np.asarray(x, np.float32).astype(ml_dtypes.bfloat16).astype(np.float64), axis, -1)
    blocks = v.reshape(v.shape[:-1] + (-1, 32))
    amax = np.abs(blocks).max(-1, keepdims=True)
    byte = np.maximum(np.where(amax > 0, np.frexp(amax)[1] - 1 + 127, 0) - down, 1)
    scale = np.exp2(byte - 127.0)
    codes = (blocks / scale).astype(np.float32).astype(dtype).astype(np.float64)
    return np.moveaxis((codes * scale).reshape(v.shape), -1, axis)


WIDE = False


def mx_kscale(k):
    if not WIDE:
        return np.ones(k)
    levels = np.array([10, -10, 5, -5, 0])
    if k % 512:
        return np.exp2(np.random.permutation(np.resize(levels, k // 32))).repeat(32)
    a = np.empty((k // 512, 16))
    for p in range(k // 512):
        a[p, :8] = np.random.permutation(np.resize(levels, 8))
        for g in range(8):
            far = levels[np.abs(levels - a[p, g]) >= 10]
            a[p, g + 8] = far[np.random.randint(len(far))]
    return np.exp2(a.ravel()).repeat(32)


BF16 = ml_dtypes.bfloat16


def bf(x):
    return np.asarray(x, np.float32).astype(BF16)


def f64(x):
    return np.asarray(x).astype(np.float64)


B, H, W, C, F, K, G, RR = 2, 16, 16, 16384, 256, 3, 16, 4
KK = K * K
P = B * H * W


def setup_inputs():
    s = mx_kscale(C)
    return {"x": bf(np.random.standard_normal((B, H, W, C)) * s),
            "Wi": bf(np.random.standard_normal((C, F)) / np.sqrt(C) / s[:, None]),
            "bi": bf(np.random.standard_normal(F) * 0.3),
            "w_span": bf(np.random.standard_normal((B, H, W, KK * G)) * 0.7)}


def reference(x, Wi, bi, w_span):
    xi = ((mxq(f64(x).reshape(P, C), 1, "e4m3") @ mxq(f64(Wi), 0, "e4m3")) + f64(bi)).reshape(B, H, W, F)
    pad = (K - 1) // 2
    xp = np.pad(xi, ((0, 0), (pad, pad), (pad, pad), (0, 0)))
    patches = np.stack([xp[:, i:i + H, j:j + W, :] for i in range(K) for j in range(K)], axis=-2)
    patches = patches.reshape(B, H, W, G, F // G, KK)
    w = f64(w_span).reshape(B, H, W, G, KK)[:, :, :, :, None, :]
    return (w * patches).sum(-1).reshape(B, H, W, F)

@@ -1,0 +1,301 @@
+from contextlib import ExitStack
+
+import concourse.mybir as mybir
+from concourse.masks import make_identity
+
+F32 = mybir.dt.float32
+BF16 = mybir.dt.bfloat16
+U32 = mybir.dt.uint32
+U8 = mybir.dt.uint8
+FP8X4 = mybir.dt.float8_e4m3fn_x4
+ALU = mybir.AluOpType
+ACT = mybir.ActivationFunctionType
+AXIS = mybir.AxisListType
+
+P = 128
+IMAGES = 2
+SIDE = 16
+IMG_PIX = SIDE * SIDE
+HALVES = IMG_PIX // P
+C_IN = 16384
+F_OUT = 256
+F_TILES = F_OUT // P
+PACK = 4
+K_PASS = P * PACK
+PASS_WORDS = K_PASS // 2
+PASSES = C_IN // K_PASS
+ROUND = 4
+ROUNDS = PASSES // ROUND
+CHUNK_ROUNDS = 2
+CHUNK_K = CHUNK_ROUNDS * ROUND * K_PASS
+LOAD_AHEAD = 4
+
+TAPS = 9
+GROUPS = 16
+GROUP_CH = F_OUT // GROUPS
+WIN_GROUPS = 2
+WIN = WIN_GROUPS * GROUP_CH * TAPS
+WINDOWS = GROUPS // WIN_GROUPS
+WIN_BLOCKS = 3
+IMG_WINDOWS = HALVES * WINDOWS
+STEP_WINDOWS = 3
+XI_LEFT = 32
+XI_WIDTH = 320
+
+FLOPS = 2 * IMAGES * IMG_PIX * C_IN * F_OUT
+
+
+def tile_involution2d_pa_k_kernel(tc, x, Wi, bi, w_span, out):
+    nc = tc.nc
+    x_rows = x.rearrange("b u v k -> (b u v) k")
+    out_rows = out.rearrange("b u v o -> (b u v) o")
+    wi_rows = Wi.rearrange("(g p t) c -> p g (t c)", p=P, t=PACK)
+
+    with ExitStack() as ctx:
+        const = ctx.enter_context(tc.tile_pool(name="const", bufs=1))
+        x_pool = ctx.enter_context(tc.tile_pool(name="x_pool", bufs=3))
+        wi_raw_pool = ctx.enter_context(tc.tile_pool(name="wi_raw_pool", bufs=LOAD_AHEAD + 1))
+        wi_grp_pool = ctx.enter_context(tc.tile_pool(name="wi_grp_pool", bufs=2))
+        x_grp_pool = ctx.enter_context(tc.tile_pool(name="x_grp_pool", bufs=3))
+        x_mx_pool = ctx.enter_context(tc.tile_pool(name="x_mx_pool", bufs=3))
+        products_pool = ctx.enter_context(tc.tile_pool(name="products_pool", bufs=1))
+        result_pool = ctx.enter_context(tc.tile_pool(name="result_pool", bufs=2))
+        patch_sb_pool = ctx.enter_context(tc.tile_pool(name="patch_sb_pool", bufs=3))
+        acc_pool = ctx.enter_context(tc.psum_pool(name="acc_pool", bufs=1))
+        work_pool = ctx.enter_context(tc.psum_pool(name="work_pool", bufs=6))
+        ctx.enter_context(tc.manual_schedule())
+
+        ident = const.tile([P, P], F32)
+        make_identity(nc, ident[:])
+
+        w_sb = const.tile([P, IMAGES * HALVES, GROUPS * TAPS], BF16)
+        nc.scalar.dma_start(
+            out=w_sb[:],
+            in_=w_span.rearrange("b u v q -> (b u v) q").rearrange("(r p) q -> p r q", p=P),
+        )
+
+        bias_rows = const.tile([P, P], BF16)
+        nc.vector.memset(bias_rows[:], 0.0)
+        bias_col = const.tile([P, F_TILES], F32)
+        nc.scalar.activation(out=bias_col[:], in_=bias_rows[:, 0:F_TILES], func=ACT.Identity)
+        nc.scalar.dma_start(out=bias_rows[0:F_TILES, :], in_=bi.rearrange("(f c) -> f c", f=F_TILES))
+        bias_rows32 = const.tile([P, P], F32)
+
+        def transpose_bias():
+            nc.vector.tensor_copy(out=bias_rows32[:], in_=bias_rows[:])
+            flipped = work_pool.tile([P, P], F32, tag="work")
+            nc.tensor.transpose(flipped[:], bias_rows32[:], ident[:])
+            nc.vector.tensor_copy(out=bias_col[:], in_=flipped[:, 0:F_TILES])
+
+        xi_copies = []
+        for b in range(IMAGES):
+            xi = const.tile([P, 3, F_TILES, XI_WIDTH], F32, name="xi%d" % b)
+            nc.vector.memset(xi[:], 0.0)
+            xi_copies.append(xi)
+
+        wi_codes = const.tile([P, PASSES * F_OUT], U32, align_bytes=64)
+        wi_scales = const.tile([P, PASSES * F_OUT], U8, align_bytes=64)
+
+        wi_raw = {}
+        x_chunks = {}
+
+        def issue_loads(step):
+            if step % CHUNK_ROUNDS == 0:
+                chunk = step // CHUNK_ROUNDS
+                b, part = divmod(chunk, ROUNDS // CHUNK_ROUNDS)
+                x_chunk = x_pool.tile([P, HALVES, CHUNK_K], BF16)
+                for h in range(HALVES):
+                    first_pixel = (b * HALVES + h) * P
+                    nc.sync.dma_start(
+                        out=x_chunk[:, h, :],
+                        in_=x_rows[first_pixel : first_pixel + P, part * CHUNK_K : (part + 1) * CHUNK_K],
+                    )
+                x_chunks[chunk] = x_chunk
+            if step < ROUNDS:
+                raw = wi_raw_pool.tile([P, ROUND, PACK, F_OUT], BF16)
+                nc.sync.dma_start(
+                    out=raw[:].rearrange("p g t c -> p g (t c)"),
+                    in_=wi_rows[:, ROUND * step : ROUND * (step + 1), :],
+                )
+                wi_raw[step] = raw
+
+        def regroup_wi(kr):
+            raw = wi_raw[kr]
+            grouped = wi_grp_pool.tile([P, ROUND, F_OUT, PACK], BF16, align_bytes=64)
+            for g in range(ROUND):
+                dst = grouped[:, g, :, :].rearrange("p (c i) t -> p c t i", i=4)
+                src = raw[:, g, :, :].rearrange("p t (c i) -> p c t i", i=4)
+                if g < ROUND - 1:
+                    nc.vector.tensor_copy(out=dst, in_=src)
+                else:
+                    nc.scalar.copy(out=dst, in_=src)
+            return grouped
+
+        def quantise_wi(kr, grouped):
+            cols = slice(kr * ROUND * F_OUT, (kr + 1) * ROUND * F_OUT)
+            nc.vector.quantize_mx(
+                out=wi_codes[:, cols].bitcast(FP8X4),
+                scales=wi_scales[:, cols],
+                in_=grouped[:].rearrange("p g c t -> p (g c t)"),
+            )
+
+        def transpose_x(step):
+            x_chunk = x_chunks[step // CHUNK_ROUNDS]
+            grouped = x_grp_pool.tile([P, ROUND * IMG_PIX * PACK], BF16, align_bytes=64)
+            grouped_words = grouped[:].bitcast(F32)
+            for g in range(ROUND):
+                first_word = ((step % CHUNK_ROUNDS) * ROUND + g) * PASS_WORDS
+                bank = work_pool.tile([P, 2, IMG_PIX], F32, tag="work")
+                for u in range(2):
+                    for h in range(HALVES):
+                        nc.tensor.transpose(
+                            bank[:, u, h * P : (h + 1) * P],
+                            x_chunk[:, h, :].bitcast(F32)[:, first_word + u : first_word + PASS_WORDS : 2],
+                            ident[:],
+                        )
+                nc.scalar.copy(
+                    out=grouped_words[:, g * 2 * IMG_PIX : (g + 1) * 2 * IMG_PIX].rearrange(
+                        "p (r u) -> p r u", u=2
+                    ),
+                    in_=bank[:].rearrange("p u r -> p r u"),
+                )
+            return grouped
+
+        def quantise_x(grouped):
+            codes = x_mx_pool.tile([P, ROUND * IMG_PIX], U32, align_bytes=64)
+            scales = x_mx_pool.tile([P, ROUND * IMG_PIX], U8, align_bytes=64)
+            nc.vector.quantize_mx(out=codes[:].bitcast(FP8X4), scales=scales[:], in_=grouped[:])
+            return codes, scales
+
+        def multiply(kr, acc, codes, scales):
+            for g in range(ROUND):
+                k_pass = kr * ROUND + g
+                pixels = slice(g * IMG_PIX, (g + 1) * IMG_PIX)
+                for f in range(F_TILES):
+                    columns = slice(k_pass * F_OUT + f * P, k_pass * F_OUT + (f + 1) * P)
+                    nc.tensor.matmul_mx(
+                        out=acc[f][:],
+                        lhsT=wi_codes[:, columns].bitcast(FP8X4),
+                        lhsT_scale=wi_scales[:, columns],
+                        rhs=codes[:, pixels].bitcast(FP8X4),
+                        rhs_scale=scales[:, pixels],
+                        start=(k_pass == 0),
+                        stop=(k_pass == PASSES - 1),
+                    )
+
+        def spread_xi(b, acc):
+            xi = xi_copies[b]
+            for f in range(F_TILES):
+                image = acc[f][:].rearrange("p (u v) -> p u v", v=SIDE)
+                for j in range(3):
+                    v_lo = max(0, j - 1)
+                    v_hi = min(SIDE, SIDE - 1 + j)
+                    first = XI_LEFT - (j - 1)
+                    dst = xi[:, j, f, first : first + IMG_PIX].rearrange("p (u v) -> p u v", v=SIDE)
+                    if f == 0:
+                        nc.scalar.activation(
+                            out=dst[:, :, v_lo:v_hi],
+                            in_=image[:, :, v_lo:v_hi],
+                            func=ACT.Identity,
+                            bias=bias_col[:, f : f + 1],
+                            scale=1.0,
+                        )
+                    else:
+                        nc.vector.tensor_scalar(
+                            out=dst[:, :, v_lo:v_hi],
+                            in0=image[:, :, v_lo:v_hi],
+                            scalar1=bias_col[:, f : f + 1],
+                            scalar2=None,
+                            op0=ALU.add,
+                        )
+
+        def weigh_window(b, e, products):
+            xi = xi_copies[b]
+            h, wd = divmod(e, WINDOWS)
+            first_block = (WIN * wd) // P
+            skip = WIN * wd - first_block * P
+            patch = work_pool.tile([P, WIN_BLOCKS * P], F32, tag="work")
+            for s in range(WIN_BLOCKS):
+                t, f = divmod(first_block + s, F_TILES)
+                i, j = divmod(t, 3)
+                start = XI_LEFT + h * P + (i - 1) * SIDE
+                nc.tensor.transpose(patch[:, s * P : (s + 1) * P], xi[:, j, f, start : start + P], ident[:])
+            weights = (
+                w_sb[:, b * HALVES + h, WIN_GROUPS * TAPS * wd : WIN_GROUPS * TAPS * (wd + 1)]
+                .rearrange("p (g m) -> p g m", m=TAPS)
+                .unsqueeze(2)
+                .to_broadcast([P, WIN_GROUPS, GROUP_CH, TAPS])
+            )
+            weighed = products[:, WIN * e : WIN * (e + 1)].rearrange("p (g c m) -> p g c m", g=WIN_GROUPS, m=TAPS)
+            if e % 3 != 1:
+                nc.vector.tensor_tensor(
+                    out=weighed,
+                    in0=patch[:, skip : skip + WIN].rearrange("p (g c m) -> p g c m", g=WIN_GROUPS, m=TAPS),
+                    in1=weights,
+                    op=ALU.mult,
+                )
+            else:
+                patch_sb = patch_sb_pool.tile([P, WIN], F32)
+                nc.scalar.copy(out=patch_sb[:], in_=patch[:, skip : skip + WIN])
+                nc.gpsimd.tensor_tensor(
+                    out=weighed,
+                    in0=patch_sb[:].rearrange("p (g c m) -> p g c m", g=WIN_GROUPS, m=TAPS),
+                    in1=weights,
+                    op=ALU.mult,
+                )
+
+        def sum_windows(b, first, count, products, result):
+            outputs = WIN // TAPS
+            nc.vector.tensor_reduce(
+                out=result[:, outputs * first : outputs * (first + count)],
+                in_=products[:, WIN * first : WIN * (first + count)].rearrange("p (o m) -> p o m", m=TAPS),
+                axis=AXIS.X,
+                op=ALU.add,
+            )
+            for h in range(HALVES):
+                if first < WINDOWS * (h + 1) <= first + count:
+                    first_pixel = (b * HALVES + h) * P
+                    nc.sync.dma_start(
+                        out=out_rows[first_pixel : first_pixel + P, :], in_=result[:, h * F_OUT : (h + 1) * F_OUT]
+                    )
+
+        steps = IMAGES * ROUNDS
+        for step in range(LOAD_AHEAD):
+            issue_loads(step)
+        x_grouped = transpose_x(0)
+        wi_grouped = regroup_wi(0)
+        transpose_bias()
+        acc = None
+        products = None
+        result = None
+        for step in range(steps):
+            b, kr = divmod(step, ROUNDS)
+            if step + LOAD_AHEAD < steps:
+                issue_loads(step + LOAD_AHEAD)
+            if kr == 0:
+                acc = [acc_pool.tile([P, IMG_PIX], F32, name="acc%d" % f) for f in range(F_TILES)]
+            codes, scales = quantise_x(x_grouped)
+            if b == 0:
+                quantise_wi(kr, wi_grouped)
+            if step + 1 < steps:
+                x_grouped = transpose_x(step + 1)
+            if step + 1 < ROUNDS:
+                wi_grouped = regroup_wi(step + 1)
+            if b == 1:
+                if kr == 0:
+                    products = products_pool.tile([P, IMG_WINDOWS * WIN], F32)
+                    result = result_pool.tile([P, HALVES * F_OUT], F32)
+                summed = (kr - 1) * STEP_WINDOWS
+                if 0 <= summed < IMG_WINDOWS:
+                    sum_windows(0, summed, min(STEP_WINDOWS, IMG_WINDOWS - summed), products, result)
+                for e in range(kr * STEP_WINDOWS, min((kr + 1) * STEP_WINDOWS, IMG_WINDOWS)):
+                    weigh_window(0, e, products)
+            multiply(kr, acc, codes, scales)
+            if kr == ROUNDS - 1:
+                spread_xi(b, acc)
+        products = products_pool.tile([P, IMG_WINDOWS * WIN], F32)
+        result = result_pool.tile([P, HALVES * F_OUT], F32)
+        for e in range(IMG_WINDOWS):
+            weigh_window(1, e, products)
+        for h in range(HALVES):
+            sum_windows(1, h * WINDOWS, WINDOWS, products, result)

@@ -24,23 +24,27 @@ PACK = 4
 K_PASS = P * PACK
 PASS_WORDS = K_PASS // 2
 PASSES = C_IN // K_PASS
-ROUND = 4
-ROUNDS = PASSES // ROUND
-CHUNK_ROUNDS = 2
-CHUNK_K = CHUNK_ROUNDS * ROUND * K_PASS
-LOAD_AHEAD = 4
+UNIT = 4
+UNIT_K = UNIT * K_PASS
+UNITS = PASSES // UNIT
+STEP = 2
+STEPS = PASSES // STEP
+BANK = 512
 
 TAPS = 9
 GROUPS = 16
 GROUP_CH = F_OUT // GROUPS
 WIN_GROUPS = 2
 WIN = WIN_GROUPS * GROUP_CH * TAPS
+WIN_OUT = WIN // TAPS
 WINDOWS = GROUPS // WIN_GROUPS
 WIN_BLOCKS = 3
-IMG_WINDOWS = HALVES * WINDOWS
-STEP_WINDOWS = 3
+EARLY_WINDOWS = 2 * WINDOWS * HALVES // 2 + (6 * F_OUT) // WIN
+ALL_WINDOWS = IMAGES * HALVES * WINDOWS
+TURN_WINDOWS = 3
 XI_LEFT = 32
 XI_WIDTH = 320
+WI_VECTOR = 96
 
 FLOPS = 2 * IMAGES * IMG_PIX * C_IN * F_OUT
 
@@ -53,38 +57,91 @@ def tile_involution2d_pa_k_kernel(tc, x, Wi, bi, w_span, out):
 
     with ExitStack() as ctx:
         const = ctx.enter_context(tc.tile_pool(name="const", bufs=1))
-        x_pool = ctx.enter_context(tc.tile_pool(name="x_pool", bufs=3))
-        wi_raw_pool = ctx.enter_context(tc.tile_pool(name="wi_raw_pool", bufs=LOAD_AHEAD + 1))
+        pair_pool = ctx.enter_context(tc.tile_pool(name="pair_pool", bufs=4))
+        half_pool = ctx.enter_context(tc.tile_pool(name="half_pool", bufs=4))
+        wi_raw_pool = ctx.enter_context(tc.tile_pool(name="wi_raw_pool", bufs=4))
         wi_grp_pool = ctx.enter_context(tc.tile_pool(name="wi_grp_pool", bufs=2))
-        x_grp_pool = ctx.enter_context(tc.tile_pool(name="x_grp_pool", bufs=3))
-        x_mx_pool = ctx.enter_context(tc.tile_pool(name="x_mx_pool", bufs=3))
-        products_pool = ctx.enter_context(tc.tile_pool(name="products_pool", bufs=1))
-        result_pool = ctx.enter_context(tc.tile_pool(name="result_pool", bufs=2))
+        grp_pool = ctx.enter_context(tc.tile_pool(name="grp_pool", bufs=3))
+        mx_pool = ctx.enter_context(tc.tile_pool(name="mx_pool", bufs=3))
+        products_pool = ctx.enter_context(tc.tile_pool(name="products_pool", bufs=3))
         patch_sb_pool = ctx.enter_context(tc.tile_pool(name="patch_sb_pool", bufs=3))
-        acc_pool = ctx.enter_context(tc.psum_pool(name="acc_pool", bufs=1))
-        work_pool = ctx.enter_context(tc.psum_pool(name="work_pool", bufs=6))
+        psum = ctx.enter_context(tc.psum_pool(name="psum", bufs=1))
         ctx.enter_context(tc.manual_schedule())
+
+        turn = [0]
+
+        def bank(tag):
+            return psum.tile([P, BANK], F32, name=tag, tag=tag)
+
+        def work_bank(tags):
+            turn[0] += 1
+            return bank(tags[turn[0] % len(tags)])
+
+        WORK_A = ["work%d" % i for i in range(4)]
+        WORK_B = WORK_A + ["half0", "half1"]
+        WORK_C = WORK_B + ["pair0", "pair1"]
+
+        pair_raw = {}
+        half_raw = {}
+        wi_raw = {}
+
+        def load_pixels(raw, slot, tile_index, first, passes):
+            k0 = first * K_PASS
+            o0 = (first % UNIT) * K_PASS
+            width = passes * K_PASS
+            nc.sync.dma_start(
+                out=raw[:, slot, o0 : o0 + width],
+                in_=x_rows[tile_index * P : (tile_index + 1) * P, k0 : k0 + width],
+            )
+
+        def load_first_phase(unit, pieces):
+            pair = pair_pool.tile([P, HALVES, UNIT_K], BF16, name="pair")
+            half = half_pool.tile([P, 1, UNIT_K], BF16, name="half")
+            raw = wi_raw_pool.tile([P, UNIT, PACK, F_OUT], BF16, name="raw")
+            count = UNIT // pieces
+            for piece in range(pieces):
+                first = unit * UNIT + piece * count
+                for h in range(HALVES):
+                    load_pixels(pair, h, h, first, count)
+                load_pixels(half, 0, 2, first, count)
+                nc.sync.dma_start(
+                    out=raw[:, piece * count : (piece + 1) * count, :, :].rearrange("p g t c -> p g (t c)"),
+                    in_=wi_rows[:, first : first + count, :],
+                )
+            pair_raw[unit] = pair
+            half_raw[unit] = half
+            wi_raw[unit] = raw
+
+        def load_second_phase(unit):
+            half = half_pool.tile([P, 1, UNIT_K], BF16, name="half")
+            load_pixels(half, 0, 3, unit * UNIT, UNIT)
+            half_raw[UNITS + unit] = half
+
+        load_first_phase(0, 2)
+        load_first_phase(1, 1)
+        load_first_phase(2, 1)
 
         ident = const.tile([P, P], F32)
         make_identity(nc, ident[:])
-
-        w_sb = const.tile([P, IMAGES * HALVES, GROUPS * TAPS], BF16)
-        nc.scalar.dma_start(
-            out=w_sb[:],
-            in_=w_span.rearrange("b u v q -> (b u v) q").rearrange("(r p) q -> p r q", p=P),
-        )
 
         bias_rows = const.tile([P, P], BF16)
         nc.vector.memset(bias_rows[:], 0.0)
         bias_col = const.tile([P, F_TILES], F32)
         nc.scalar.activation(out=bias_col[:], in_=bias_rows[:, 0:F_TILES], func=ACT.Identity)
-        nc.scalar.dma_start(out=bias_rows[0:F_TILES, :], in_=bi.rearrange("(f c) -> f c", f=F_TILES))
         bias_rows32 = const.tile([P, P], F32)
+        w_sb = const.tile([P, IMAGES * HALVES, GROUPS * TAPS], BF16)
+
+        def load_small():
+            nc.sync.dma_start(out=bias_rows[0:F_TILES, :], in_=bi.rearrange("(f c) -> f c", f=F_TILES))
+            nc.sync.dma_start(
+                out=w_sb[:],
+                in_=w_span.rearrange("b u v q -> (b u v) q").rearrange("(r p) q -> p r q", p=P),
+            )
 
         def transpose_bias():
             nc.vector.tensor_copy(out=bias_rows32[:], in_=bias_rows[:])
-            flipped = work_pool.tile([P, P], F32, tag="work")
-            nc.tensor.transpose(flipped[:], bias_rows32[:], ident[:])
+            flipped = work_bank(WORK_A)
+            nc.tensor.transpose(flipped[:, 0:P], bias_rows32[:], ident[:])
             nc.vector.tensor_copy(out=bias_col[:], in_=flipped[:, 0:F_TILES])
 
         xi_copies = []
@@ -95,103 +152,87 @@ def tile_involution2d_pa_k_kernel(tc, x, Wi, bi, w_span, out):
 
         wi_codes = const.tile([P, PASSES * F_OUT], U32, align_bytes=64)
         wi_scales = const.tile([P, PASSES * F_OUT], U8, align_bytes=64)
+        result = const.tile([P, ALL_WINDOWS * WIN_OUT], F32)
 
-        wi_raw = {}
-        x_chunks = {}
-
-        def issue_loads(step):
-            if step % CHUNK_ROUNDS == 0:
-                chunk = step // CHUNK_ROUNDS
-                b, part = divmod(chunk, ROUNDS // CHUNK_ROUNDS)
-                x_chunk = x_pool.tile([P, HALVES, CHUNK_K], BF16)
-                for h in range(HALVES):
-                    first_pixel = (b * HALVES + h) * P
-                    nc.sync.dma_start(
-                        out=x_chunk[:, h, :],
-                        in_=x_rows[first_pixel : first_pixel + P, part * CHUNK_K : (part + 1) * CHUNK_K],
-                    )
-                x_chunks[chunk] = x_chunk
-            if step < ROUNDS:
-                raw = wi_raw_pool.tile([P, ROUND, PACK, F_OUT], BF16)
-                nc.sync.dma_start(
-                    out=raw[:].rearrange("p g t c -> p g (t c)"),
-                    in_=wi_rows[:, ROUND * step : ROUND * (step + 1), :],
-                )
-                wi_raw[step] = raw
-
-        def regroup_wi(kr):
-            raw = wi_raw[kr]
-            grouped = wi_grp_pool.tile([P, ROUND, F_OUT, PACK], BF16, align_bytes=64)
-            for g in range(ROUND):
+        def regroup_wi(first):
+            raw = wi_raw[first // UNIT]
+            grouped = wi_grp_pool.tile([P, STEP, F_OUT, PACK], BF16, align_bytes=64, name="wi_grp")
+            for g in range(STEP):
                 dst = grouped[:, g, :, :].rearrange("p (c i) t -> p c t i", i=4)
-                src = raw[:, g, :, :].rearrange("p t (c i) -> p c t i", i=4)
-                if g < ROUND - 1:
-                    nc.vector.tensor_copy(out=dst, in_=src)
-                else:
-                    nc.scalar.copy(out=dst, in_=src)
+                src = raw[:, (first + g) % UNIT, :, :].rearrange("p t (c i) -> p c t i", i=4)
+                split = (F_OUT if g < STEP - 1 else WI_VECTOR) // 4
+                nc.vector.tensor_copy(out=dst[:, :split], in_=src[:, :split])
+                if split < F_OUT // 4:
+                    nc.scalar.copy(out=dst[:, split:], in_=src[:, split:])
             return grouped
 
-        def quantise_wi(kr, grouped):
-            cols = slice(kr * ROUND * F_OUT, (kr + 1) * ROUND * F_OUT)
+        def quantise_wi(first, grouped):
+            cols = slice(first * F_OUT, (first + STEP) * F_OUT)
             nc.vector.quantize_mx(
                 out=wi_codes[:, cols].bitcast(FP8X4),
                 scales=wi_scales[:, cols],
                 in_=grouped[:].rearrange("p g c t -> p (g c t)"),
             )
 
-        def transpose_x(step):
-            x_chunk = x_chunks[step // CHUNK_ROUNDS]
-            grouped = x_grp_pool.tile([P, ROUND * IMG_PIX * PACK], BF16, align_bytes=64)
-            grouped_words = grouped[:].bitcast(F32)
-            for g in range(ROUND):
-                first_word = ((step % CHUNK_ROUNDS) * ROUND + g) * PASS_WORDS
-                bank = work_pool.tile([P, 2, IMG_PIX], F32, tag="work")
-                for u in range(2):
-                    for h in range(HALVES):
-                        nc.tensor.transpose(
-                            bank[:, u, h * P : (h + 1) * P],
-                            x_chunk[:, h, :].bitcast(F32)[:, first_word + u : first_word + PASS_WORDS : 2],
-                            ident[:],
-                        )
+        def transpose_x(raw, slots, first, passes, tag, tags):
+            pixels = slots * P
+            bank_passes = BANK // (2 * pixels)
+            grouped = grp_pool.tile([P, passes, pixels * PACK], BF16, align_bytes=64, name=tag, tag=tag)
+            words = grouped[:].rearrange("p g n -> p (g n)").bitcast(F32)
+            for g0 in range(0, passes, bank_passes):
+                flipped = work_bank(tags)
+                for g in range(bank_passes):
+                    first_word = ((first + g0 + g) % UNIT) * PASS_WORDS
+                    for u in range(2):
+                        for h in range(slots):
+                            col = (g * 2 + u) * pixels + h * P
+                            nc.tensor.transpose(
+                                flipped[:, col : col + P],
+                                raw[:, h, :].bitcast(F32)[:, first_word + u : first_word + PASS_WORDS : 2],
+                                ident[:],
+                            )
                 nc.scalar.copy(
-                    out=grouped_words[:, g * 2 * IMG_PIX : (g + 1) * 2 * IMG_PIX].rearrange(
-                        "p (r u) -> p r u", u=2
+                    out=words[:, g0 * 2 * pixels : g0 * 2 * pixels + BANK].rearrange(
+                        "p (g r u) -> p g r u", g=bank_passes, u=2
                     ),
-                    in_=bank[:].rearrange("p u r -> p r u"),
+                    in_=flipped[:].rearrange("p (g u r) -> p g r u", g=bank_passes, u=2),
                 )
             return grouped
 
-        def quantise_x(grouped):
-            codes = x_mx_pool.tile([P, ROUND * IMG_PIX], U32, align_bytes=64)
-            scales = x_mx_pool.tile([P, ROUND * IMG_PIX], U8, align_bytes=64)
-            nc.vector.quantize_mx(out=codes[:].bitcast(FP8X4), scales=scales[:], in_=grouped[:])
+        def quantise_x(grouped, passes, pixels, tag):
+            codes = mx_pool.tile([P, passes * pixels], U32, align_bytes=64, name=tag + "c", tag=tag + "c")
+            scales = mx_pool.tile([P, passes * pixels], U8, align_bytes=64, name=tag + "s", tag=tag + "s")
+            nc.vector.quantize_mx(
+                out=codes[:].bitcast(FP8X4), scales=scales[:], in_=grouped[:].rearrange("p g n -> p (g n)")
+            )
             return codes, scales
 
-        def multiply(kr, acc, codes, scales):
-            for g in range(ROUND):
-                k_pass = kr * ROUND + g
-                pixels = slice(g * IMG_PIX, (g + 1) * IMG_PIX)
+        def multiply(first, passes, operands):
+            for g in range(passes):
+                k_pass = first + g
                 for f in range(F_TILES):
                     columns = slice(k_pass * F_OUT + f * P, k_pass * F_OUT + (f + 1) * P)
-                    nc.tensor.matmul_mx(
-                        out=acc[f][:],
-                        lhsT=wi_codes[:, columns].bitcast(FP8X4),
-                        lhsT_scale=wi_scales[:, columns],
-                        rhs=codes[:, pixels].bitcast(FP8X4),
-                        rhs_scale=scales[:, pixels],
-                        start=(k_pass == 0),
-                        stop=(k_pass == PASSES - 1),
-                    )
+                    for acc, codes, scales, pixels in operands:
+                        cols = slice(g * pixels, (g + 1) * pixels)
+                        nc.tensor.matmul_mx(
+                            out=acc[f][:, 0:pixels],
+                            lhsT=wi_codes[:, columns].bitcast(FP8X4),
+                            lhsT_scale=wi_scales[:, columns],
+                            rhs=codes[:, cols].bitcast(FP8X4),
+                            rhs_scale=scales[:, cols],
+                            start=(k_pass == 0),
+                            stop=(k_pass == PASSES - 1),
+                        )
 
-        def spread_xi(b, acc):
+        def spread_xi(b, acc, first_pixel, pixels):
             xi = xi_copies[b]
-            for f in range(F_TILES):
-                image = acc[f][:].rearrange("p (u v) -> p u v", v=SIDE)
-                for j in range(3):
-                    v_lo = max(0, j - 1)
-                    v_hi = min(SIDE, SIDE - 1 + j)
-                    first = XI_LEFT - (j - 1)
-                    dst = xi[:, j, f, first : first + IMG_PIX].rearrange("p (u v) -> p u v", v=SIDE)
+            for j in range(3):
+                v_lo = max(0, j - 1)
+                v_hi = min(SIDE, SIDE - 1 + j)
+                first = XI_LEFT + first_pixel - (j - 1)
+                for f in range(F_TILES):
+                    image = acc[f][:, 0:pixels].rearrange("p (u v) -> p u v", v=SIDE)
+                    dst = xi[:, j, f, first : first + pixels].rearrange("p (u v) -> p u v", v=SIDE)
                     if f == 0:
                         nc.scalar.activation(
                             out=dst[:, :, v_lo:v_hi],
@@ -209,25 +250,28 @@ def tile_involution2d_pa_k_kernel(tc, x, Wi, bi, w_span, out):
                             op0=ALU.add,
                         )
 
-        def weigh_window(b, e, products):
+        def weigh_window(e, products, place, tags, direct):
+            r, wd = divmod(e, WINDOWS)
+            b, h = divmod(r, HALVES)
             xi = xi_copies[b]
-            h, wd = divmod(e, WINDOWS)
             first_block = (WIN * wd) // P
             skip = WIN * wd - first_block * P
-            patch = work_pool.tile([P, WIN_BLOCKS * P], F32, tag="work")
+            patch = work_bank(tags)
             for s in range(WIN_BLOCKS):
                 t, f = divmod(first_block + s, F_TILES)
                 i, j = divmod(t, 3)
                 start = XI_LEFT + h * P + (i - 1) * SIDE
                 nc.tensor.transpose(patch[:, s * P : (s + 1) * P], xi[:, j, f, start : start + P], ident[:])
             weights = (
-                w_sb[:, b * HALVES + h, WIN_GROUPS * TAPS * wd : WIN_GROUPS * TAPS * (wd + 1)]
+                w_sb[:, r, WIN_GROUPS * TAPS * wd : WIN_GROUPS * TAPS * (wd + 1)]
                 .rearrange("p (g m) -> p g m", m=TAPS)
                 .unsqueeze(2)
                 .to_broadcast([P, WIN_GROUPS, GROUP_CH, TAPS])
             )
-            weighed = products[:, WIN * e : WIN * (e + 1)].rearrange("p (g c m) -> p g c m", g=WIN_GROUPS, m=TAPS)
-            if e % 3 != 1:
+            weighed = products[:, WIN * place : WIN * (place + 1)].rearrange(
+                "p (g c m) -> p g c m", g=WIN_GROUPS, m=TAPS
+            )
+            if direct:
                 nc.vector.tensor_tensor(
                     out=weighed,
                     in0=patch[:, skip : skip + WIN].rearrange("p (g c m) -> p g c m", g=WIN_GROUPS, m=TAPS),
@@ -244,58 +288,94 @@ def tile_involution2d_pa_k_kernel(tc, x, Wi, bi, w_span, out):
                     op=ALU.mult,
                 )
 
-        def sum_windows(b, first, count, products, result):
-            outputs = WIN // TAPS
+        def sum_windows(first, count, products):
             nc.vector.tensor_reduce(
-                out=result[:, outputs * first : outputs * (first + count)],
-                in_=products[:, WIN * first : WIN * (first + count)].rearrange("p (o m) -> p o m", m=TAPS),
+                out=result[:, WIN_OUT * first : WIN_OUT * (first + count)],
+                in_=products[:, 0 : WIN * count].rearrange("p (o m) -> p o m", m=TAPS),
                 axis=AXIS.X,
                 op=ALU.add,
             )
-            for h in range(HALVES):
-                if first < WINDOWS * (h + 1) <= first + count:
-                    first_pixel = (b * HALVES + h) * P
-                    nc.sync.dma_start(
-                        out=out_rows[first_pixel : first_pixel + P, :], in_=result[:, h * F_OUT : (h + 1) * F_OUT]
-                    )
 
-        steps = IMAGES * ROUNDS
-        for step in range(LOAD_AHEAD):
-            issue_loads(step)
-        x_grouped = transpose_x(0)
+        def store(r, lo, hi):
+            nc.sync.dma_start(
+                out=out_rows[r * P : (r + 1) * P, lo:hi], in_=result[:, r * F_OUT + lo : r * F_OUT + hi]
+            )
+
+        def transpose_step(s):
+            first = s * STEP
+            unit = first // UNIT
+            pair = transpose_x(pair_raw[unit], HALVES, first, STEP, "pair_grp", WORK_A)
+            half = transpose_x(half_raw[unit], 1, first, STEP, "half_grp", WORK_A)
+            return pair, half
+
+        grouped = transpose_step(0)
         wi_grouped = regroup_wi(0)
-        transpose_bias()
-        acc = None
-        products = None
-        result = None
-        for step in range(steps):
-            b, kr = divmod(step, ROUNDS)
-            if step + LOAD_AHEAD < steps:
-                issue_loads(step + LOAD_AHEAD)
-            if kr == 0:
-                acc = [acc_pool.tile([P, IMG_PIX], F32, name="acc%d" % f) for f in range(F_TILES)]
-            codes, scales = quantise_x(x_grouped)
-            if b == 0:
-                quantise_wi(kr, wi_grouped)
-            if step + 1 < steps:
-                x_grouped = transpose_x(step + 1)
-            if step + 1 < ROUNDS:
-                wi_grouped = regroup_wi(step + 1)
-            if b == 1:
-                if kr == 0:
-                    products = products_pool.tile([P, IMG_WINDOWS * WIN], F32)
-                    result = result_pool.tile([P, HALVES * F_OUT], F32)
-                summed = (kr - 1) * STEP_WINDOWS
-                if 0 <= summed < IMG_WINDOWS:
-                    sum_windows(0, summed, min(STEP_WINDOWS, IMG_WINDOWS - summed), products, result)
-                for e in range(kr * STEP_WINDOWS, min((kr + 1) * STEP_WINDOWS, IMG_WINDOWS)):
-                    weigh_window(0, e, products)
-            multiply(kr, acc, codes, scales)
-            if kr == ROUNDS - 1:
-                spread_xi(b, acc)
-        products = products_pool.tile([P, IMG_WINDOWS * WIN], F32)
-        result = result_pool.tile([P, HALVES * F_OUT], F32)
-        for e in range(IMG_WINDOWS):
-            weigh_window(1, e, products)
-        for h in range(HALVES):
-            sum_windows(1, h * WINDOWS, WINDOWS, products, result)
+        acc_pair = [bank("pair%d" % f) for f in range(F_TILES)]
+        acc_half = [bank("half%d" % f) for f in range(F_TILES)]
+        for s in range(STEPS):
+            if s % 2 == 0:
+                ahead = s // 2 + 3
+                if ahead < UNITS:
+                    load_first_phase(ahead, 1)
+                else:
+                    load_second_phase(ahead - UNITS)
+                if ahead == 4:
+                    load_small()
+            pair_codes, pair_scales = quantise_x(grouped[0], STEP, IMG_PIX, "pair")
+            half_codes, half_scales = quantise_x(grouped[1], STEP, P, "half")
+            quantise_wi(s * STEP, wi_grouped)
+            if s + 1 < STEPS:
+                grouped = transpose_step(s + 1)
+                wi_grouped = regroup_wi((s + 1) * STEP)
+            else:
+                last = transpose_x(half_raw[UNITS], 1, 0, UNIT, "last_grp", WORK_A)
+                last_mx = quantise_x(last, UNIT, P, "last")
+            multiply(
+                s * STEP,
+                STEP,
+                [(acc_pair, pair_codes, pair_scales, IMG_PIX), (acc_half, half_codes, half_scales, P)],
+            )
+            if s == 10:
+                transpose_bias()
+
+        spread_xi(0, acc_pair, 0, IMG_PIX)
+        spread_xi(1, acc_half, 0, P)
+        acc_last = [bank("pair%d" % f) for f in range(F_TILES)]
+        done = 0
+        pending = None
+        for unit in range(UNITS):
+            if unit + 3 < UNITS:
+                load_second_phase(unit + 3)
+            if unit + 1 < UNITS:
+                last = transpose_x(half_raw[UNITS + unit + 1], 1, (unit + 1) * UNIT, UNIT, "last_grp", WORK_B)
+            count = min(TURN_WINDOWS, EARLY_WINDOWS - done)
+            if pending:
+                sum_windows(pending[0], pending[1], pending[2])
+                for r in range(2):
+                    if pending[0] < WINDOWS * (r + 1) <= pending[0] + pending[1]:
+                        store(r, 0, F_OUT)
+                pending = None
+            if count > 0:
+                products = products_pool.tile([P, TURN_WINDOWS * WIN], F32, name="products")
+                for i in range(count):
+                    weigh_window(done + i, products, i, WORK_B, i != 1)
+                pending = (done, count, products)
+                done += count
+            multiply(unit * UNIT, UNIT, [(acc_last, last_mx[0], last_mx[1], P)])
+            if unit + 1 < UNITS:
+                last_mx = quantise_x(last, UNIT, P, "last")
+        spread_xi(1, acc_last, P, P)
+
+        for first, count in ((21, 3), (24, 3), (27, 3), (30, 2)):
+            products = products_pool.tile([P, TURN_WINDOWS * WIN], F32, name="products")
+            for i in range(count):
+                weigh_window(first + i, products, i, WORK_B, i != 1)
+            if pending:
+                sum_windows(pending[0], pending[1], pending[2])
+            if first == 27:
+                store(2, 0, F_OUT)
+            if first == 30:
+                store(3, 0, 96)
+            pending = (first, count, products)
+        sum_windows(pending[0], pending[1], pending[2])
+        store(3, 96, F_OUT)

@@ -60,7 +60,7 @@ def tile_involution2d_pa_k_kernel(tc, x, Wi, bi, w_span, out):
         pair_pool = ctx.enter_context(tc.tile_pool(name="pair_pool", bufs=4))
         half_pool = ctx.enter_context(tc.tile_pool(name="half_pool", bufs=4))
         wi_raw_pool = ctx.enter_context(tc.tile_pool(name="wi_raw_pool", bufs=4))
-        wi_grp_pool = ctx.enter_context(tc.tile_pool(name="wi_grp_pool", bufs=2))
+        wi_grp_pool = ctx.enter_context(tc.tile_pool(name="wi_grp_pool", bufs=3))
         grp_pool = ctx.enter_context(tc.tile_pool(name="grp_pool", bufs=3))
         mx_pool = ctx.enter_context(tc.tile_pool(name="mx_pool", bufs=3))
         products_pool = ctx.enter_context(tc.tile_pool(name="products_pool", bufs=3))
@@ -301,69 +301,79 @@ def tile_involution2d_pa_k_kernel(tc, x, Wi, bi, w_span, out):
                 out=out_rows[r * P : (r + 1) * P, lo:hi], in_=result[:, r * F_OUT + lo : r * F_OUT + hi]
             )
 
-        def transpose_step(s):
-            first = s * STEP
-            unit = first // UNIT
-            pair = transpose_x(pair_raw[unit], HALVES, first, STEP, "pair_grp", WORK_A)
-            half = transpose_x(half_raw[unit], 1, first, STEP, "half_grp", WORK_A)
-            return pair, half
-
-        grouped = transpose_step(0)
-        wi_grouped = regroup_wi(0)
+        turns = STEPS + UNITS
+        grouped = {}
+        wi_grouped = {}
+        operands = {}
         acc_pair = [bank("pair%d" % f) for f in range(F_TILES)]
         acc_half = [bank("half%d" % f) for f in range(F_TILES)]
-        for s in range(STEPS):
-            if s % 2 == 0:
-                ahead = s // 2 + 3
+        acc_last = []
+
+        def transpose_turn(n):
+            if n < STEPS:
+                first = n * STEP
+                unit = first // UNIT
+                pair = transpose_x(pair_raw[unit], HALVES, first, STEP, "pair_grp", WORK_A)
+                half = transpose_x(half_raw[unit], 1, first, STEP, "half_grp", WORK_A)
+                grouped[n] = (pair, half)
+                wi_grouped[n] = regroup_wi(first)
+            elif n < turns:
+                unit = n - STEPS
+                tags = WORK_A if unit < 2 else WORK_B
+                grouped[n] = transpose_x(half_raw[UNITS + unit], 1, unit * UNIT, UNIT, "last_grp", tags)
+
+        def quantise_turn(n):
+            if n < STEPS:
+                pair_codes, pair_scales = quantise_x(grouped[n][0], STEP, IMG_PIX, "pair")
+                half_codes, half_scales = quantise_x(grouped[n][1], STEP, P, "half")
+                quantise_wi(n * STEP, wi_grouped[n])
+                operands[n] = [(acc_pair, pair_codes, pair_scales, IMG_PIX), (acc_half, half_codes, half_scales, P)]
+            elif n < turns:
+                operands[n] = quantise_x(grouped[n], UNIT, P, "last")
+
+        transpose_turn(0)
+        transpose_turn(1)
+        quantise_turn(0)
+        done = 0
+        pending = None
+        for n in range(turns):
+            if n < STEPS and n % 2 == 0:
+                ahead = n // 2 + 3
                 if ahead < UNITS:
                     load_first_phase(ahead, 1)
                 else:
                     load_second_phase(ahead - UNITS)
                 if ahead == 4:
                     load_small()
-            pair_codes, pair_scales = quantise_x(grouped[0], STEP, IMG_PIX, "pair")
-            half_codes, half_scales = quantise_x(grouped[1], STEP, P, "half")
-            quantise_wi(s * STEP, wi_grouped)
-            if s + 1 < STEPS:
-                grouped = transpose_step(s + 1)
-                wi_grouped = regroup_wi((s + 1) * STEP)
+            if n >= STEPS and n - STEPS + 3 < UNITS:
+                load_second_phase(n - STEPS + 3)
+            quantise_turn(n + 1)
+            transpose_turn(n + 2)
+            if n < STEPS:
+                multiply(n * STEP, STEP, operands[n])
+                if n == 10:
+                    transpose_bias()
+                if n == STEPS - 1:
+                    spread_xi(0, acc_pair, 0, IMG_PIX)
+                    spread_xi(1, acc_half, 0, P)
+                    acc_last = [bank("pair%d" % f) for f in range(F_TILES)]
             else:
-                last = transpose_x(half_raw[UNITS], 1, 0, UNIT, "last_grp", WORK_A)
-                last_mx = quantise_x(last, UNIT, P, "last")
-            multiply(
-                s * STEP,
-                STEP,
-                [(acc_pair, pair_codes, pair_scales, IMG_PIX), (acc_half, half_codes, half_scales, P)],
-            )
-            if s == 10:
-                transpose_bias()
-
-        spread_xi(0, acc_pair, 0, IMG_PIX)
-        spread_xi(1, acc_half, 0, P)
-        acc_last = [bank("pair%d" % f) for f in range(F_TILES)]
-        done = 0
-        pending = None
-        for unit in range(UNITS):
-            if unit + 3 < UNITS:
-                load_second_phase(unit + 3)
-            if unit + 1 < UNITS:
-                last = transpose_x(half_raw[UNITS + unit + 1], 1, (unit + 1) * UNIT, UNIT, "last_grp", WORK_B)
-            count = min(TURN_WINDOWS, EARLY_WINDOWS - done)
-            if pending:
-                sum_windows(pending[0], pending[1], pending[2])
-                for r in range(2):
-                    if pending[0] < WINDOWS * (r + 1) <= pending[0] + pending[1]:
-                        store(r, 0, F_OUT)
-                pending = None
-            if count > 0:
-                products = products_pool.tile([P, TURN_WINDOWS * WIN], F32, name="products")
-                for i in range(count):
-                    weigh_window(done + i, products, i, WORK_B, i != 1)
-                pending = (done, count, products)
-                done += count
-            multiply(unit * UNIT, UNIT, [(acc_last, last_mx[0], last_mx[1], P)])
-            if unit + 1 < UNITS:
-                last_mx = quantise_x(last, UNIT, P, "last")
+                unit = n - STEPS
+                count = min(TURN_WINDOWS, EARLY_WINDOWS - done)
+                if pending:
+                    sum_windows(pending[0], pending[1], pending[2])
+                    for r in range(2):
+                        if pending[0] < WINDOWS * (r + 1) <= pending[0] + pending[1]:
+                            store(r, 0, F_OUT)
+                    pending = None
+                if count > 0:
+                    products = products_pool.tile([P, TURN_WINDOWS * WIN], F32, name="products")
+                    for i in range(count):
+                        weigh_window(done + i, products, i, WORK_B, i != 1)
+                    pending = (done, count, products)
+                    done += count
+                codes, scales = operands[n]
+                multiply(unit * UNIT, UNIT, [(acc_last, codes, scales, P)])
         spread_xi(1, acc_last, P, P)
 
         for first, count in ((21, 3), (24, 3), (27, 3), (30, 2)):

@@ -39,12 +39,34 @@ WIN = WIN_GROUPS * GROUP_CH * TAPS
 WIN_OUT = WIN // TAPS
 WINDOWS = GROUPS // WIN_GROUPS
 WIN_BLOCKS = 3
-EARLY_WINDOWS = 2 * WINDOWS * HALVES // 2 + (6 * F_OUT) // WIN
 ALL_WINDOWS = IMAGES * HALVES * WINDOWS
-TURN_WINDOWS = 3
+TURN_WINDOWS = 4
 XI_LEFT = 32
 XI_WIDTH = 320
-WI_VECTOR = 96
+WI_VECTOR = 128
+
+PARTING = (((0, "v"),), ())
+PARTING_LATE = ((0, "v"), (1, "s"))
+PART_FROM = 2
+RHYTHM = 8
+REST = (0,)
+GPS = (0, 2)
+GPS_T = (1, 3)
+WI_LAG = 1
+SMALL_TURNS = 2
+LAST_SMALL = 2
+AHEAD = 6
+PART_BUFS = 8
+GRP_BUFS = 3
+MX_BUFS = 3
+WG_BUFS = 3
+X_BUFS = 3
+W_BUFS = 3
+TLEAD = 2
+PLEAD = 4
+QLEAD = 1
+RLEAD = 2
+WLEAD = 1
 
 FLOPS = 2 * IMAGES * IMG_PIX * C_IN * F_OUT
 
@@ -57,14 +79,14 @@ def tile_involution2d_pa_k_kernel(tc, x, Wi, bi, w_span, out):
 
     with ExitStack() as ctx:
         const = ctx.enter_context(tc.tile_pool(name="const", bufs=1))
-        pair_pool = ctx.enter_context(tc.tile_pool(name="pair_pool", bufs=4))
-        half_pool = ctx.enter_context(tc.tile_pool(name="half_pool", bufs=4))
-        wi_raw_pool = ctx.enter_context(tc.tile_pool(name="wi_raw_pool", bufs=4))
-        wi_grp_pool = ctx.enter_context(tc.tile_pool(name="wi_grp_pool", bufs=3))
-        grp_pool = ctx.enter_context(tc.tile_pool(name="grp_pool", bufs=3))
-        mx_pool = ctx.enter_context(tc.tile_pool(name="mx_pool", bufs=3))
+        x_pool = ctx.enter_context(tc.tile_pool(name="x_pool", bufs=X_BUFS))
+        wi_raw_pool = ctx.enter_context(tc.tile_pool(name="wi_raw_pool", bufs=W_BUFS))
+        wi_grp_pool = ctx.enter_context(tc.tile_pool(name="wi_grp_pool", bufs=WG_BUFS))
+        grp_pool = ctx.enter_context(tc.tile_pool(name="grp_pool", bufs=GRP_BUFS))
+        part_pool = ctx.enter_context(tc.tile_pool(name="part_pool", bufs=PART_BUFS))
+        mx_pool = ctx.enter_context(tc.tile_pool(name="mx_pool", bufs=MX_BUFS))
         products_pool = ctx.enter_context(tc.tile_pool(name="products_pool", bufs=3))
-        patch_sb_pool = ctx.enter_context(tc.tile_pool(name="patch_sb_pool", bufs=3))
+        patch_sb_pool = ctx.enter_context(tc.tile_pool(name="patch_sb_pool", bufs=4))
         psum = ctx.enter_context(tc.psum_pool(name="psum", bufs=1))
         ctx.enter_context(tc.manual_schedule())
 
@@ -78,48 +100,8 @@ def tile_involution2d_pa_k_kernel(tc, x, Wi, bi, w_span, out):
             return bank(tags[turn[0] % len(tags)])
 
         WORK_A = ["work%d" % i for i in range(4)]
-        WORK_B = WORK_A + ["half0", "half1"]
-        WORK_C = WORK_B + ["pair0", "pair1"]
-
-        pair_raw = {}
-        half_raw = {}
-        wi_raw = {}
-
-        def load_pixels(raw, slot, tile_index, first, passes):
-            k0 = first * K_PASS
-            o0 = (first % UNIT) * K_PASS
-            width = passes * K_PASS
-            nc.sync.dma_start(
-                out=raw[:, slot, o0 : o0 + width],
-                in_=x_rows[tile_index * P : (tile_index + 1) * P, k0 : k0 + width],
-            )
-
-        def load_first_phase(unit, pieces):
-            pair = pair_pool.tile([P, HALVES, UNIT_K], BF16, name="pair")
-            half = half_pool.tile([P, 1, UNIT_K], BF16, name="half")
-            raw = wi_raw_pool.tile([P, UNIT, PACK, F_OUT], BF16, name="raw")
-            count = UNIT // pieces
-            for piece in range(pieces):
-                first = unit * UNIT + piece * count
-                for h in range(HALVES):
-                    load_pixels(pair, h, h, first, count)
-                load_pixels(half, 0, 2, first, count)
-                nc.sync.dma_start(
-                    out=raw[:, piece * count : (piece + 1) * count, :, :].rearrange("p g t c -> p g (t c)"),
-                    in_=wi_rows[:, first : first + count, :],
-                )
-            pair_raw[unit] = pair
-            half_raw[unit] = half
-            wi_raw[unit] = raw
-
-        def load_second_phase(unit):
-            half = half_pool.tile([P, 1, UNIT_K], BF16, name="half")
-            load_pixels(half, 0, 3, unit * UNIT, UNIT)
-            half_raw[UNITS + unit] = half
-
-        load_first_phase(0, 2)
-        load_first_phase(1, 1)
-        load_first_phase(2, 1)
+        WORK_B = WORK_A + ["acc00", "acc01"]
+        WORK_C = WORK_B + ["acc10", "acc11"]
 
         ident = const.tile([P, P], F32)
         make_identity(nc, ident[:])
@@ -128,21 +110,82 @@ def tile_involution2d_pa_k_kernel(tc, x, Wi, bi, w_span, out):
         nc.vector.memset(bias_rows[:], 0.0)
         bias_col = const.tile([P, F_TILES], F32)
         nc.scalar.activation(out=bias_col[:], in_=bias_rows[:, 0:F_TILES], func=ACT.Identity)
+        nc.scalar.dma_start(out=bias_rows[0:F_TILES, :], in_=bi.rearrange("(f c) -> f c", f=F_TILES))
         bias_rows32 = const.tile([P, P], F32)
-        w_sb = const.tile([P, IMAGES * HALVES, GROUPS * TAPS], BF16)
-
-        def load_small():
-            nc.sync.dma_start(out=bias_rows[0:F_TILES, :], in_=bi.rearrange("(f c) -> f c", f=F_TILES))
-            nc.sync.dma_start(
-                out=w_sb[:],
-                in_=w_span.rearrange("b u v q -> (b u v) q").rearrange("(r p) q -> p r q", p=P),
-            )
 
         def transpose_bias():
             nc.vector.tensor_copy(out=bias_rows32[:], in_=bias_rows[:])
             flipped = work_bank(WORK_A)
             nc.tensor.transpose(flipped[:, 0:P], bias_rows32[:], ident[:])
             nc.vector.tensor_copy(out=bias_col[:], in_=flipped[:, 0:F_TILES])
+
+        w_sb = const.tile([P, IMAGES * HALVES, GROUPS * TAPS], BF16)
+
+        def load_weights():
+            nc.sync.dma_start(
+                out=w_sb[:],
+                in_=w_span.rearrange("b u v q -> (b u v) q").rearrange("(r p) q -> p r q", p=P),
+            )
+
+        x_raw = {}
+        wi_raw = {}
+
+        def load_pixels(b, raw, first, count):
+            o0 = (first % UNIT) * K_PASS
+            for h in range(HALVES):
+                row = (b * HALVES + h) * P
+                nc.sync.dma_start(
+                    out=raw[:, h, o0 : o0 + count * K_PASS],
+                    in_=x_rows[row : row + P, first * K_PASS : (first + count) * K_PASS],
+                )
+
+        def load_wi(raw, first, count):
+            g0 = first % UNIT
+            nc.sync.dma_start(
+                out=raw[:, g0 : g0 + count, :, :].rearrange("p g t c -> p g (t c)"),
+                in_=wi_rows[:, first : first + count, :],
+            )
+
+        turn_steps = []
+        m1 = 0
+        while m1 < STEPS:
+            n = len(turn_steps)
+            joins = n >= STEPS or n % RHYTHM not in REST
+            turn_steps.append((n if n < STEPS else None, m1 if joins else None))
+            m1 += joins
+        turns = len(turn_steps)
+
+        load_queue = []
+        for n in range(turns + WI_LAG):
+            if n < turns:
+                for b in range(IMAGES):
+                    m = turn_steps[n][b]
+                    if m is not None:
+                        if m < SMALL_TURNS:
+                            load_queue.append((n, b, m * STEP, STEP))
+                        elif (m * STEP) % UNIT == 0:
+                            load_queue.append((n, b, m * STEP, UNIT))
+            w = n - WI_LAG
+            if 0 <= w < STEPS:
+                if w < SMALL_TURNS or w >= STEPS - LAST_SMALL:
+                    load_queue.append((n, 2, w * STEP, STEP))
+                elif (w * STEP) % UNIT == 0:
+                    load_queue.append((n, 2, w * STEP, UNIT))
+
+        def issue_loads(n):
+            while load_queue and load_queue[0][0] <= n:
+                need, what, first, count = load_queue.pop(0)
+                unit = first // UNIT
+                if what < 2:
+                    if (what, unit) not in x_raw:
+                        x_raw[what, unit] = x_pool.tile([P, HALVES, UNIT_K], BF16, name="x%d" % what, tag="x%d" % what)
+                    load_pixels(what, x_raw[what, unit], first, count)
+                else:
+                    if unit not in wi_raw:
+                        wi_raw[unit] = wi_raw_pool.tile([P, UNIT, PACK, F_OUT], BF16, name="raw")
+                    load_wi(wi_raw[unit], first, count)
+
+        issue_loads(AHEAD - 1)
 
         xi_copies = []
         for b in range(IMAGES):
@@ -174,65 +217,68 @@ def tile_involution2d_pa_k_kernel(tc, x, Wi, bi, w_span, out):
                 in_=grouped[:].rearrange("p g c t -> p (g c t)"),
             )
 
-        def transpose_x(raw, slots, first, passes, tag, tags):
-            pixels = slots * P
-            bank_passes = BANK // (2 * pixels)
-            grouped = grp_pool.tile([P, passes, pixels * PACK], BF16, align_bytes=64, name=tag, tag=tag)
-            words = grouped[:].rearrange("p g n -> p (g n)").bitcast(F32)
-            for g0 in range(0, passes, bank_passes):
+        def part_words(raw, h, first, engine):
+            o0 = (first % UNIT) * PASS_WORDS
+            parted = part_pool.tile([P, 2, STEP * P], F32, name="parted", tag="parted")
+            src = raw[:, h, :].bitcast(F32)[:, o0 : o0 + STEP * PASS_WORDS].rearrange("p (w u) -> p u w", u=2)
+            if engine == "v":
+                nc.vector.tensor_copy(out=parted[:], in_=src)
+            else:
+                nc.scalar.copy(out=parted[:], in_=src)
+            return parted
+
+        def transpose_x(raw, parted, first, tag, tags):
+            grouped = grp_pool.tile([P, STEP, IMG_PIX * PACK], BF16, align_bytes=64, name=tag, tag=tag)
+            for g in range(STEP):
                 flipped = work_bank(tags)
-                for g in range(bank_passes):
-                    first_word = ((first + g0 + g) % UNIT) * PASS_WORDS
-                    for u in range(2):
-                        for h in range(slots):
-                            col = (g * 2 + u) * pixels + h * P
-                            nc.tensor.transpose(
-                                flipped[:, col : col + P],
-                                raw[:, h, :].bitcast(F32)[:, first_word + u : first_word + PASS_WORDS : 2],
-                                ident[:],
-                            )
+                first_word = ((first + g) % UNIT) * PASS_WORDS
+                for u in range(2):
+                    for h in range(HALVES):
+                        col = u * IMG_PIX + h * P
+                        if h in parted:
+                            words = parted[h][:, u, g * P : (g + 1) * P]
+                        else:
+                            words = raw[:, h, :].bitcast(F32)[:, first_word + u : first_word + PASS_WORDS : 2]
+                        nc.tensor.transpose(flipped[:, col : col + P], words, ident[:])
                 nc.scalar.copy(
-                    out=words[:, g0 * 2 * pixels : g0 * 2 * pixels + BANK].rearrange(
-                        "p (g r u) -> p g r u", g=bank_passes, u=2
-                    ),
-                    in_=flipped[:].rearrange("p (g u r) -> p g r u", g=bank_passes, u=2),
+                    out=grouped[:, g, :].bitcast(F32).rearrange("p (r u) -> p r u", u=2),
+                    in_=flipped[:].rearrange("p (u r) -> p r u", u=2),
                 )
             return grouped
 
-        def quantise_x(grouped, passes, pixels, tag):
-            codes = mx_pool.tile([P, passes * pixels], U32, align_bytes=64, name=tag + "c", tag=tag + "c")
-            scales = mx_pool.tile([P, passes * pixels], U8, align_bytes=64, name=tag + "s", tag=tag + "s")
+        def quantise_x(grouped, tag):
+            codes = mx_pool.tile([P, STEP * IMG_PIX], U32, align_bytes=64, name=tag + "c", tag=tag + "c")
+            scales = mx_pool.tile([P, STEP * IMG_PIX], U8, align_bytes=64, name=tag + "s", tag=tag + "s")
             nc.vector.quantize_mx(
                 out=codes[:].bitcast(FP8X4), scales=scales[:], in_=grouped[:].rearrange("p g n -> p (g n)")
             )
             return codes, scales
 
-        def multiply(first, passes, operands):
-            for g in range(passes):
+        def multiply(first, acc, codes, scales):
+            for g in range(STEP):
                 k_pass = first + g
+                cols = slice(g * IMG_PIX, (g + 1) * IMG_PIX)
                 for f in range(F_TILES):
                     columns = slice(k_pass * F_OUT + f * P, k_pass * F_OUT + (f + 1) * P)
-                    for acc, codes, scales, pixels in operands:
-                        cols = slice(g * pixels, (g + 1) * pixels)
-                        nc.tensor.matmul_mx(
-                            out=acc[f][:, 0:pixels],
-                            lhsT=wi_codes[:, columns].bitcast(FP8X4),
-                            lhsT_scale=wi_scales[:, columns],
-                            rhs=codes[:, cols].bitcast(FP8X4),
-                            rhs_scale=scales[:, cols],
-                            start=(k_pass == 0),
-                            stop=(k_pass == PASSES - 1),
-                        )
+                    nc.tensor.matmul_mx(
+                        out=acc[f][:, 0:IMG_PIX],
+                        lhsT=wi_codes[:, columns].bitcast(FP8X4),
+                        lhsT_scale=wi_scales[:, columns],
+                        rhs=codes[:, cols].bitcast(FP8X4),
+                        rhs_scale=scales[:, cols],
+                        start=(k_pass == 0),
+                        stop=(k_pass == PASSES - 1),
+                    )
 
-        def spread_xi(b, acc, first_pixel, pixels):
+        def spread_xi(b, acc):
             xi = xi_copies[b]
             for j in range(3):
                 v_lo = max(0, j - 1)
                 v_hi = min(SIDE, SIDE - 1 + j)
-                first = XI_LEFT + first_pixel - (j - 1)
+                first = XI_LEFT - (j - 1)
                 for f in range(F_TILES):
-                    image = acc[f][:, 0:pixels].rearrange("p (u v) -> p u v", v=SIDE)
-                    dst = xi[:, j, f, first : first + pixels].rearrange("p (u v) -> p u v", v=SIDE)
+                    image = acc[f][:, 0:IMG_PIX].rearrange("p (u v) -> p u v", v=SIDE)
+                    dst = xi[:, j, f, first : first + IMG_PIX].rearrange("p (u v) -> p u v", v=SIDE)
                     if f == 0:
                         nc.scalar.activation(
                             out=dst[:, :, v_lo:v_hi],
@@ -301,91 +347,89 @@ def tile_involution2d_pa_k_kernel(tc, x, Wi, bi, w_span, out):
                 out=out_rows[r * P : (r + 1) * P, lo:hi], in_=result[:, r * F_OUT + lo : r * F_OUT + hi]
             )
 
-        turns = STEPS + UNITS
+        acc = [[bank("acc%d%d" % (b, f)) for f in range(F_TILES)] for b in range(IMAGES)]
         grouped = {}
         wi_grouped = {}
-        operands = {}
-        acc_pair = [bank("pair%d" % f) for f in range(F_TILES)]
-        acc_half = [bank("half%d" % f) for f in range(F_TILES)]
-        acc_last = []
+        mx = {}
 
-        def transpose_turn(n):
-            if n < STEPS:
-                first = n * STEP
-                unit = first // UNIT
-                pair = transpose_x(pair_raw[unit], HALVES, first, STEP, "pair_grp", WORK_A)
-                half = transpose_x(half_raw[unit], 1, first, STEP, "half_grp", WORK_A)
-                grouped[n] = (pair, half)
-                wi_grouped[n] = regroup_wi(first)
-            elif n < turns:
-                unit = n - STEPS
-                tags = WORK_A if unit < 2 else WORK_B
-                grouped[n] = transpose_x(half_raw[UNITS + unit], 1, unit * UNIT, UNIT, "last_grp", tags)
+        def step_images(n):
+            return [(b, m) for b, m in enumerate(turn_steps[n]) if m is not None] if n < turns else []
 
-        def quantise_turn(n):
+        def transpose_step(n):
+            tags = WORK_A if n < STEPS + TLEAD else WORK_B
+            for b, m in step_images(n):
+                grouped[b, m] = transpose_x(x_raw[b, m * STEP // UNIT], parted.get((b, m), {}), m * STEP, "x%dg" % b, tags)
+
+        def regroup_step(n):
             if n < STEPS:
-                pair_codes, pair_scales = quantise_x(grouped[n][0], STEP, IMG_PIX, "pair")
-                half_codes, half_scales = quantise_x(grouped[n][1], STEP, P, "half")
+                wi_grouped[n] = regroup_wi(n * STEP)
+
+        parted = {}
+
+        def part_step(n):
+            for b, m in step_images(n):
+                who = PARTING[b] if n < STEPS else PARTING_LATE
+                if n < PART_FROM:
+                    who = []
+                parted[b, m] = {h: part_words(x_raw[b, m * STEP // UNIT], h, m * STEP, e) for h, e in who}
+
+        def quantise_step(n):
+            for b, m in step_images(n):
+                mx[b, m] = quantise_x(grouped[b, m], "x%d" % b)
+
+        def quantise_wi_step(n):
+            if n < STEPS:
                 quantise_wi(n * STEP, wi_grouped[n])
-                operands[n] = [(acc_pair, pair_codes, pair_scales, IMG_PIX), (acc_half, half_codes, half_scales, P)]
-            elif n < turns:
-                operands[n] = quantise_x(grouped[n], UNIT, P, "last")
 
-        transpose_turn(0)
-        transpose_turn(1)
-        quantise_turn(0)
-        done = 0
-        pending = None
-        for n in range(turns):
-            if n < STEPS and n % 2 == 0:
-                ahead = n // 2 + 3
-                if ahead < UNITS:
-                    load_first_phase(ahead, 1)
-                else:
-                    load_second_phase(ahead - UNITS)
-                if ahead == 4:
-                    load_small()
-            if n >= STEPS and n - STEPS + 3 < UNITS:
-                load_second_phase(n - STEPS + 3)
-            quantise_turn(n + 1)
-            transpose_turn(n + 2)
-            if n < STEPS:
-                multiply(n * STEP, STEP, operands[n])
-                if n == 10:
-                    transpose_bias()
-                if n == STEPS - 1:
-                    spread_xi(0, acc_pair, 0, IMG_PIX)
-                    spread_xi(1, acc_half, 0, P)
-                    acc_last = [bank("pair%d" % f) for f in range(F_TILES)]
-            else:
-                unit = n - STEPS
-                count = min(TURN_WINDOWS, EARLY_WINDOWS - done)
-                if pending:
-                    sum_windows(pending[0], pending[1], pending[2])
-                    for r in range(2):
-                        if pending[0] < WINDOWS * (r + 1) <= pending[0] + pending[1]:
-                            store(r, 0, F_OUT)
-                    pending = None
-                if count > 0:
-                    products = products_pool.tile([P, TURN_WINDOWS * WIN], F32, name="products")
-                    for i in range(count):
-                        weigh_window(done + i, products, i, WORK_B, i != 1)
-                    pending = (done, count, products)
-                    done += count
-                codes, scales = operands[n]
-                multiply(unit * UNIT, UNIT, [(acc_last, codes, scales, P)])
-        spread_xi(1, acc_last, P, P)
-
-        for first, count in ((21, 3), (24, 3), (27, 3), (30, 2)):
+        def weigh_windows(first, tags, gps):
             products = products_pool.tile([P, TURN_WINDOWS * WIN], F32, name="products")
-            for i in range(count):
-                weigh_window(first + i, products, i, WORK_B, i != 1)
-            if pending:
-                sum_windows(pending[0], pending[1], pending[2])
-            if first == 27:
-                store(2, 0, F_OUT)
-            if first == 30:
-                store(3, 0, 96)
-            pending = (first, count, products)
-        sum_windows(pending[0], pending[1], pending[2])
-        store(3, 96, F_OUT)
+            for i in range(TURN_WINDOWS):
+                weigh_window(first + i, products, i, tags, i not in gps)
+            return first, products
+
+        def finish_windows(first, products):
+            sum_windows(first, TURN_WINDOWS, products)
+            r, wd = divmod(first, WINDOWS)
+            store(r, WIN_OUT * wd, WIN_OUT * (wd + TURN_WINDOWS))
+
+        for n in range(PLEAD - TLEAD):
+            part_step(n)
+        for n in range(TLEAD):
+            transpose_step(n)
+            if n == 0:
+                transpose_bias()
+            part_step(n + PLEAD - TLEAD)
+            if n < QLEAD:
+                quantise_step(n)
+        for n in range(RLEAD):
+            regroup_step(n)
+            if n < WLEAD:
+                quantise_wi_step(n)
+        waiting = None
+        done = 0
+        for n in range(turns):
+            issue_loads(n + AHEAD)
+            if n == 4:
+                load_weights()
+            quantise_step(n + QLEAD)
+            quantise_wi_step(n + WLEAD)
+            transpose_step(n + TLEAD)
+            regroup_step(n + RLEAD)
+            part_step(n + PLEAD)
+            for b, m in step_images(n):
+                multiply(m * STEP, acc[b], mx[b, m][0], mx[b, m][1])
+            if n == STEPS - 1:
+                spread_xi(0, acc[0])
+            if n == turns - 1:
+                spread_xi(1, acc[1])
+            if n >= STEPS and done < HALVES * WINDOWS:
+                if waiting:
+                    finish_windows(waiting[0], waiting[1])
+                waiting = weigh_windows(done, WORK_B, GPS)
+                done += TURN_WINDOWS
+        for first in range(done, ALL_WINDOWS, TURN_WINDOWS):
+            following = weigh_windows(first, WORK_C, GPS_T)
+            if waiting:
+                finish_windows(waiting[0], waiting[1])
+            waiting = following
+        finish_windows(waiting[0], waiting[1])

@@ -132,12 +132,16 @@ def tile_involution2d_pa_k_kernel(tc, x, Wi, bi, w_span, out):
 
         def load_pixels(b, raw, first, count):
             o0 = (first % UNIT) * K_PASS
-            for h in range(HALVES):
-                row = (b * HALVES + h) * P
+            image = x_rows[b * IMG_PIX : (b + 1) * IMG_PIX, first * K_PASS : (first + count) * K_PASS]
+            if count == UNIT:
                 nc.sync.dma_start(
-                    out=raw[:, h, o0 : o0 + count * K_PASS],
-                    in_=x_rows[row : row + P, first * K_PASS : (first + count) * K_PASS],
+                    out=raw[:, :, o0 : o0 + count * K_PASS], in_=image.rearrange("(h p) k -> p h k", p=P)
                 )
+            else:
+                for h in range(HALVES):
+                    nc.sync.dma_start(
+                        out=raw[:, h, o0 : o0 + count * K_PASS], in_=image[h * P : (h + 1) * P, :]
+                    )
 
         def load_wi(raw, first, count):
             g0 = first % UNIT

@@ -45,7 +45,7 @@ XI_LEFT = 32
 XI_WIDTH = 320
 WI_VECTOR = 128
 
-PARTING = (((0, "v"),), ())
+PARTING = ((), ())
 PARTING_LATE = ((0, "v"), (1, "s"))
 PART_FROM = 2
 RHYTHM = 8

@@ -165,7 +165,7 @@ def tile_involution2d_pa_k_kernel(tc, x, Wi, bi, w_span, out):
                 for b in range(IMAGES):
                     m = turn_steps[n][b]
                     if m is not None:
-                        if m < SMALL_TURNS:
+                        if m < SMALL_TURNS or m >= STEPS - LAST_SMALL:
                             load_queue.append((n, b, m * STEP, STEP))
                         elif (m * STEP) % UNIT == 0:
                             load_queue.append((n, b, m * STEP, UNIT))
@@ -427,9 +427,10 @@ def tile_involution2d_pa_k_kernel(tc, x, Wi, bi, w_span, out):
             if n == turns - 1:
                 spread_xi(1, acc[1])
             if n >= STEPS and done < HALVES * WINDOWS:
+                following = weigh_windows(done, WORK_B, GPS)
                 if waiting:
                     finish_windows(waiting[0], waiting[1])
-                waiting = weigh_windows(done, WORK_B, GPS)
+                waiting = following
                 done += TURN_WINDOWS
         for first in range(done, ALL_WINDOWS, TURN_WINDOWS):
             following = weigh_windows(first, WORK_C, GPS_T)

@@ -165,7 +165,7 @@ def tile_involution2d_pa_k_kernel(tc, x, Wi, bi, w_span, out):
                 for b in range(IMAGES):
                     m = turn_steps[n][b]
                     if m is not None:
-                        if m < SMALL_TURNS or m >= STEPS - LAST_SMALL:
+                        if m >= STEPS - LAST_SMALL:
                             load_queue.append((n, b, m * STEP, STEP))
                         elif (m * STEP) % UNIT == 0:
                             load_queue.append((n, b, m * STEP, UNIT))
@@ -413,7 +413,7 @@ def tile_involution2d_pa_k_kernel(tc, x, Wi, bi, w_span, out):
         done = 0
         for n in range(turns):
             issue_loads(n + AHEAD)
-            if n == 4:
+            if n == turns + WI_LAG - 1 - AHEAD:
                 load_weights()
             quantise_step(n + QLEAD)
             quantise_wi_step(n + WLEAD)

@@ -109,8 +109,9 @@ def tile_involution2d_pa_k_kernel(tc, x, Wi, bi, w_span, out):
         bias_rows = const.tile([P, P], BF16)
         nc.vector.memset(bias_rows[:], 0.0)
         bias_col = const.tile([P, F_TILES], F32)
-        nc.scalar.activation(out=bias_col[:], in_=bias_rows[:, 0:F_TILES], func=ACT.Identity)
-        nc.scalar.dma_start(out=bias_rows[0:F_TILES, :], in_=bi.rearrange("(f c) -> f c", f=F_TILES))
+        warm = const.tile([P, 1], F32)
+        nc.vector.memset(warm[:], 0.0)
+        nc.scalar.activation(out=warm[:], in_=warm[:], func=ACT.Identity)
         bias_rows32 = const.tile([P, P], F32)
 
         def transpose_bias():
@@ -189,6 +190,8 @@ def tile_involution2d_pa_k_kernel(tc, x, Wi, bi, w_span, out):
                         wi_raw[unit] = wi_raw_pool.tile([P, UNIT, PACK, F_OUT], BF16, name="raw")
                     load_wi(wi_raw[unit], first, count)
 
+        issue_loads(0)
+        nc.sync.dma_start(out=bias_rows[0:F_TILES, :], in_=bi.rearrange("(f c) -> f c", f=F_TILES))
         issue_loads(AHEAD - 1)
 
         xi_copies = []
@@ -207,7 +210,7 @@ def tile_involution2d_pa_k_kernel(tc, x, Wi, bi, w_span, out):
             for g in range(STEP):
                 dst = grouped[:, g, :, :].rearrange("p (c i) t -> p c t i", i=4)
                 src = raw[:, (first + g) % UNIT, :, :].rearrange("p t (c i) -> p c t i", i=4)
-                split = (F_OUT if g < STEP - 1 else WI_VECTOR) // 4
+                split = (F_OUT if g < STEP - 1 or first == PASSES - STEP else WI_VECTOR) // 4
                 nc.vector.tensor_copy(out=dst[:, :split], in_=src[:, :split])
                 if split < F_OUT // 4:
                     nc.scalar.copy(out=dst[:, split:], in_=src[:, split:])
@@ -377,9 +380,10 @@ def tile_involution2d_pa_k_kernel(tc, x, Wi, bi, w_span, out):
                     who = []
                 parted[b, m] = {h: part_words(x_raw[b, m * STEP // UNIT], h, m * STEP, e) for h, e in who}
 
-        def quantise_step(n):
+        def quantise_step(n, image):
             for b, m in step_images(n):
-                mx[b, m] = quantise_x(grouped[b, m], "x%d" % b)
+                if b == image:
+                    mx[b, m] = quantise_x(grouped[b, m], "x%d" % b)
 
         def quantise_wi_step(n):
             if n < STEPS:
@@ -404,7 +408,8 @@ def tile_involution2d_pa_k_kernel(tc, x, Wi, bi, w_span, out):
                 transpose_bias()
             part_step(n + PLEAD - TLEAD)
             if n < QLEAD:
-                quantise_step(n)
+                for b in range(IMAGES):
+                    quantise_step(n, b)
         for n in range(RLEAD):
             regroup_step(n)
             if n < WLEAD:
@@ -415,8 +420,9 @@ def tile_involution2d_pa_k_kernel(tc, x, Wi, bi, w_span, out):
             issue_loads(n + AHEAD)
             if n == turns + WI_LAG - 1 - AHEAD:
                 load_weights()
-            quantise_step(n + QLEAD)
+            quantise_step(n + QLEAD, 0)
             quantise_wi_step(n + WLEAD)
+            quantise_step(n + QLEAD, 1)
             transpose_step(n + TLEAD)
             regroup_step(n + RLEAD)
             part_step(n + PLEAD)

@@ -43,15 +43,19 @@ ALL_WINDOWS = IMAGES * HALVES * WINDOWS
 TURN_WINDOWS = 4
 XI_LEFT = 32
 XI_WIDTH = 320
-WI_VECTOR = 128
+WI_VECTOR = 64
 
-PARTING = ((), ())
+PARTING = (((0, "v"),), ())
 PARTING_LATE = ((0, "v"), (1, "s"))
 PART_FROM = 2
 RHYTHM = 8
 REST = (0,)
-GPS = (0, 2)
-GPS_T = (1, 3)
+TENSOR_SUM = 4
+GPS = (1, 3)
+GPS_SPREAD = (1,)
+GPS_SUM = (0, 1, 3)
+GPS_REST = (1,)
+GPS_OF = {1: GPS_SPREAD, TENSOR_SUM: GPS_SUM, TENSOR_SUM + 1: GPS_REST}
 WI_LAG = 1
 SMALL_TURNS = 2
 LAST_SMALL = 2
@@ -85,7 +89,7 @@ def tile_involution2d_pa_k_kernel(tc, x, Wi, bi, w_span, out):
         grp_pool = ctx.enter_context(tc.tile_pool(name="grp_pool", bufs=GRP_BUFS))
         part_pool = ctx.enter_context(tc.tile_pool(name="part_pool", bufs=PART_BUFS))
         mx_pool = ctx.enter_context(tc.tile_pool(name="mx_pool", bufs=MX_BUFS))
-        products_pool = ctx.enter_context(tc.tile_pool(name="products_pool", bufs=3))
+        products_pool = ctx.enter_context(tc.tile_pool(name="products_pool", bufs=5))
         patch_sb_pool = ctx.enter_context(tc.tile_pool(name="patch_sb_pool", bufs=4))
         psum = ctx.enter_context(tc.psum_pool(name="psum", bufs=1))
         ctx.enter_context(tc.manual_schedule())
@@ -286,7 +290,7 @@ def tile_involution2d_pa_k_kernel(tc, x, Wi, bi, w_span, out):
                 for f in range(F_TILES):
                     image = acc[f][:, 0:IMG_PIX].rearrange("p (u v) -> p u v", v=SIDE)
                     dst = xi[:, j, f, first : first + IMG_PIX].rearrange("p (u v) -> p u v", v=SIDE)
-                    if f == 0:
+                    if f == 0 or (b == 1 and j == 2):
                         nc.scalar.activation(
                             out=dst[:, :, v_lo:v_hi],
                             in_=image[:, :, v_lo:v_hi],
@@ -303,7 +307,7 @@ def tile_involution2d_pa_k_kernel(tc, x, Wi, bi, w_span, out):
                             op0=ALU.add,
                         )
 
-        def weigh_window(e, products, place, tags, direct):
+        def weigh_window(e, products, place, tags, direct, by_tap):
             r, wd = divmod(e, WINDOWS)
             b, h = divmod(r, HALVES)
             xi = xi_copies[b]
@@ -315,31 +319,55 @@ def tile_involution2d_pa_k_kernel(tc, x, Wi, bi, w_span, out):
                 i, j = divmod(t, 3)
                 start = XI_LEFT + h * P + (i - 1) * SIDE
                 nc.tensor.transpose(patch[:, s * P : (s + 1) * P], xi[:, j, f, start : start + P], ident[:])
-            weights = (
-                w_sb[:, r, WIN_GROUPS * TAPS * wd : WIN_GROUPS * TAPS * (wd + 1)]
-                .rearrange("p (g m) -> p g m", m=TAPS)
-                .unsqueeze(2)
-                .to_broadcast([P, WIN_GROUPS, GROUP_CH, TAPS])
-            )
-            weighed = products[:, WIN * place : WIN * (place + 1)].rearrange(
-                "p (g c m) -> p g c m", g=WIN_GROUPS, m=TAPS
-            )
+            weights = w_sb[:, r, WIN_GROUPS * TAPS * wd : WIN_GROUPS * TAPS * (wd + 1)]
+            if by_tap:
+                order = "p (g c m) -> p m g c"
+                weights = (
+                    weights.rearrange("p (g m) -> p m g", m=TAPS)
+                    .unsqueeze(3)
+                    .to_broadcast([P, TAPS, WIN_GROUPS, GROUP_CH])
+                )
+                weighed = products.rearrange("p (m o) -> p m o", m=TAPS)[:, :, WIN_OUT * place : WIN_OUT * (place + 1)]
+                weighed = weighed.rearrange("p m (g c) -> p m g c", g=WIN_GROUPS)
+            else:
+                order = "p (g c m) -> p g c m"
+                weights = (
+                    weights.rearrange("p (g m) -> p g m", m=TAPS)
+                    .unsqueeze(2)
+                    .to_broadcast([P, WIN_GROUPS, GROUP_CH, TAPS])
+                )
+                weighed = products[:, WIN * place : WIN * (place + 1)].rearrange(
+                    "p (g c m) -> p g c m", g=WIN_GROUPS, m=TAPS
+                )
+            entries = patch[:, skip : skip + WIN]
             if direct:
                 nc.vector.tensor_tensor(
-                    out=weighed,
-                    in0=patch[:, skip : skip + WIN].rearrange("p (g c m) -> p g c m", g=WIN_GROUPS, m=TAPS),
-                    in1=weights,
-                    op=ALU.mult,
+                    out=weighed, in0=entries.rearrange(order, g=WIN_GROUPS, m=TAPS), in1=weights, op=ALU.mult
                 )
             else:
                 patch_sb = patch_sb_pool.tile([P, WIN], F32)
-                nc.scalar.copy(out=patch_sb[:], in_=patch[:, skip : skip + WIN])
+                nc.scalar.copy(out=patch_sb[:], in_=entries)
                 nc.gpsimd.tensor_tensor(
-                    out=weighed,
-                    in0=patch_sb[:].rearrange("p (g c m) -> p g c m", g=WIN_GROUPS, m=TAPS),
-                    in1=weights,
-                    op=ALU.mult,
+                    out=weighed, in0=patch_sb[:].rearrange(order, g=WIN_GROUPS, m=TAPS), in1=weights, op=ALU.mult
                 )
+
+        def add_nines(products, bank_tile):
+            for m in range(TAPS):
+                nc.tensor.matmul(
+                    bank_tile[:, 0:P],
+                    lhsT=products[:, m * P : (m + 1) * P],
+                    rhs=ident[:],
+                    is_transpose=True,
+                    start=(m == 0),
+                    stop=(m == TAPS - 1),
+                )
+            sums_sb = patch_sb_pool.tile([P, P], F32, name="sums_sb")
+            nc.scalar.copy(out=sums_sb[:], in_=bank_tile[:, 0:P])
+            return sums_sb
+
+        def turn_back(first, sums_sb, bank_tile):
+            nc.tensor.transpose(bank_tile[:, 0:P], sums_sb[:], ident[:])
+            nc.scalar.copy(out=result[:, WIN_OUT * first : WIN_OUT * first + P], in_=bank_tile[:, 0:P])
 
         def sum_windows(first, count, products):
             nc.vector.tensor_reduce(
@@ -389,16 +417,21 @@ def tile_involution2d_pa_k_kernel(tc, x, Wi, bi, w_span, out):
             if n < STEPS:
                 quantise_wi(n * STEP, wi_grouped[n])
 
-        def weigh_windows(first, tags, gps):
+        def weigh_windows(first, tags):
+            group = first // TURN_WINDOWS
+            gps = GPS_OF.get(group, GPS)
             products = products_pool.tile([P, TURN_WINDOWS * WIN], F32, name="products")
             for i in range(TURN_WINDOWS):
-                weigh_window(first + i, products, i, tags, i not in gps)
+                weigh_window(first + i, products[:], i, tags, i not in gps, group == TENSOR_SUM)
             return first, products
+
+        def store_windows(first):
+            r, wd = divmod(first, WINDOWS)
+            store(r, WIN_OUT * wd, WIN_OUT * (wd + TURN_WINDOWS))
 
         def finish_windows(first, products):
             sum_windows(first, TURN_WINDOWS, products)
-            r, wd = divmod(first, WINDOWS)
-            store(r, WIN_OUT * wd, WIN_OUT * (wd + TURN_WINDOWS))
+            store_windows(first)
 
         for n in range(PLEAD - TLEAD):
             part_step(n)
@@ -433,14 +466,20 @@ def tile_involution2d_pa_k_kernel(tc, x, Wi, bi, w_span, out):
             if n == turns - 1:
                 spread_xi(1, acc[1])
             if n >= STEPS and done < HALVES * WINDOWS:
-                following = weigh_windows(done, WORK_B, GPS)
+                following = weigh_windows(done, WORK_B)
                 if waiting:
                     finish_windows(waiting[0], waiting[1])
                 waiting = following
                 done += TURN_WINDOWS
+        for_tensor = None
         for first in range(done, ALL_WINDOWS, TURN_WINDOWS):
-            following = weigh_windows(first, WORK_C, GPS_T)
-            if waiting:
+            following = weigh_windows(first, WORK_C)
+            if waiting[0] // TURN_WINDOWS == TENSOR_SUM:
+                for_tensor = waiting
+            else:
                 finish_windows(waiting[0], waiting[1])
             waiting = following
+        sums_sb = add_nines(for_tensor[1][:], work_bank(WORK_C))
+        turn_back(for_tensor[0], sums_sb, work_bank(WORK_C))
+        store_windows(for_tensor[0])
         finish_windows(waiting[0], waiting[1])

from contextlib import ExitStack

import concourse.mybir as mybir
from concourse.masks import make_identity

F32 = mybir.dt.float32
BF16 = mybir.dt.bfloat16
U32 = mybir.dt.uint32
U8 = mybir.dt.uint8
FP8X4 = mybir.dt.float8_e4m3fn_x4
ALU = mybir.AluOpType
ACT = mybir.ActivationFunctionType
AXIS = mybir.AxisListType

P = 128
IMAGES = 2
SIDE = 16
IMG_PIX = SIDE * SIDE
HALVES = IMG_PIX // P
C_IN = 16384
F_OUT = 256
F_TILES = F_OUT // P
PACK = 4
K_PASS = P * PACK
PASS_WORDS = K_PASS // 2
PASSES = C_IN // K_PASS
UNIT = 4
UNIT_K = UNIT * K_PASS
UNITS = PASSES // UNIT
STEP = 2
STEPS = PASSES // STEP
BANK = 512

TAPS = 9
GROUPS = 16
GROUP_CH = F_OUT // GROUPS
WIN_GROUPS = 2
WIN = WIN_GROUPS * GROUP_CH * TAPS
WIN_OUT = WIN // TAPS
WINDOWS = GROUPS // WIN_GROUPS
WIN_BLOCKS = 3
ALL_WINDOWS = IMAGES * HALVES * WINDOWS
TURN_WINDOWS = 4
XI_LEFT = 32
XI_WIDTH = 320
WI_VECTOR = 64

PARTING = (((0, "v"),), ())
PARTING_LATE = ((0, "v"), (1, "s"))
PART_FROM = 2
RHYTHM = 8
REST = (0,)
TENSOR_SUM = 4
GPS = (1, 3)
GPS_SPREAD = (1,)
GPS_SUM = (0, 1, 3)
GPS_REST = (1,)
GPS_OF = {1: GPS_SPREAD, TENSOR_SUM: GPS_SUM, TENSOR_SUM + 1: GPS_REST}
WI_LAG = 1
SMALL_TURNS = 2
LAST_SMALL = 2
AHEAD = 6
PART_BUFS = 8
GRP_BUFS = 3
MX_BUFS = 3
WG_BUFS = 3
X_BUFS = 3
W_BUFS = 3
TLEAD = 2
PLEAD = 4
QLEAD = 1
RLEAD = 2
WLEAD = 1

FLOPS = 2 * IMAGES * IMG_PIX * C_IN * F_OUT


def tile_involution2d_pa_k_kernel(tc, x, Wi, bi, w_span, out):
    nc = tc.nc
    x_rows = x.rearrange("b u v k -> (b u v) k")
    out_rows = out.rearrange("b u v o -> (b u v) o")
    wi_rows = Wi.rearrange("(g p t) c -> p g (t c)", p=P, t=PACK)

    with ExitStack() as ctx:
        const = ctx.enter_context(tc.tile_pool(name="const", bufs=1))
        x_pool = ctx.enter_context(tc.tile_pool(name="x_pool", bufs=X_BUFS))
        wi_raw_pool = ctx.enter_context(tc.tile_pool(name="wi_raw_pool", bufs=W_BUFS))
        wi_grp_pool = ctx.enter_context(tc.tile_pool(name="wi_grp_pool", bufs=WG_BUFS))
        grp_pool = ctx.enter_context(tc.tile_pool(name="grp_pool", bufs=GRP_BUFS))
        part_pool = ctx.enter_context(tc.tile_pool(name="part_pool", bufs=PART_BUFS))
        mx_pool = ctx.enter_context(tc.tile_pool(name="mx_pool", bufs=MX_BUFS))
        products_pool = ctx.enter_context(tc.tile_pool(name="products_pool", bufs=5))
        patch_sb_pool = ctx.enter_context(tc.tile_pool(name="patch_sb_pool", bufs=4))
        psum = ctx.enter_context(tc.psum_pool(name="psum", bufs=1))
        ctx.enter_context(tc.manual_schedule())

        turn = [0]

        def bank(tag):
            return psum.tile([P, BANK], F32, name=tag, tag=tag)

        def work_bank(tags):
            turn[0] += 1
            return bank(tags[turn[0] % len(tags)])

        WORK_A = ["work%d" % i for i in range(4)]
        WORK_B = WORK_A + ["acc00", "acc01"]
        WORK_C = WORK_B + ["acc10", "acc11"]

        ident = const.tile([P, P], F32)
        make_identity(nc, ident[:])

        bias_rows = const.tile([P, P], BF16)
        nc.vector.memset(bias_rows[:], 0.0)
        bias_col = const.tile([P, F_TILES], F32)
        warm = const.tile([P, 1], F32)
        nc.vector.memset(warm[:], 0.0)
        nc.scalar.activation(out=warm[:], in_=warm[:], func=ACT.Identity)
        bias_rows32 = const.tile([P, P], F32)

        def transpose_bias():
            nc.vector.tensor_copy(out=bias_rows32[:], in_=bias_rows[:])
            flipped = work_bank(WORK_A)
            nc.tensor.transpose(flipped[:, 0:P], bias_rows32[:], ident[:])
            nc.vector.tensor_copy(out=bias_col[:], in_=flipped[:, 0:F_TILES])

        w_sb = const.tile([P, IMAGES * HALVES, GROUPS * TAPS], BF16)

        def load_weights():
            nc.sync.dma_start(
                out=w_sb[:],
                in_=w_span.rearrange("b u v q -> (b u v) q").rearrange("(r p) q -> p r q", p=P),
            )

        x_raw = {}
        wi_raw = {}

        def load_pixels(b, raw, first, count):
            o0 = (first % UNIT) * K_PASS
            image = x_rows[b * IMG_PIX : (b + 1) * IMG_PIX, first * K_PASS : (first + count) * K_PASS]
            if count == UNIT:
                nc.sync.dma_start(
                    out=raw[:, :, o0 : o0 + count * K_PASS], in_=image.rearrange("(h p) k -> p h k", p=P)
                )
            else:
                for h in range(HALVES):
                    nc.sync.dma_start(
                        out=raw[:, h, o0 : o0 + count * K_PASS], in_=image[h * P : (h + 1) * P, :]
                    )

        def load_wi(raw, first, count):
            g0 = first % UNIT
            nc.sync.dma_start(
                out=raw[:, g0 : g0 + count, :, :].rearrange("p g t c -> p g (t c)"),
                in_=wi_rows[:, first : first + count, :],
            )

        turn_steps = []
        m1 = 0
        while m1 < STEPS:
            n = len(turn_steps)
            joins = n >= STEPS or n % RHYTHM not in REST
            turn_steps.append((n if n < STEPS else None, m1 if joins else None))
            m1 += joins
        turns = len(turn_steps)

        load_queue = []
        for n in range(turns + WI_LAG):
            if n < turns:
                for b in range(IMAGES):
                    m = turn_steps[n][b]
                    if m is not None:
                        if m >= STEPS - LAST_SMALL:
                            load_queue.append((n, b, m * STEP, STEP))
                        elif (m * STEP) % UNIT == 0:
                            load_queue.append((n, b, m * STEP, UNIT))
            w = n - WI_LAG
            if 0 <= w < STEPS:
                if w < SMALL_TURNS or w >= STEPS - LAST_SMALL:
                    load_queue.append((n, 2, w * STEP, STEP))
                elif (w * STEP) % UNIT == 0:
                    load_queue.append((n, 2, w * STEP, UNIT))

        def issue_loads(n):
            while load_queue and load_queue[0][0] <= n:
                need, what, first, count = load_queue.pop(0)
                unit = first // UNIT
                if what < 2:
                    if (what, unit) not in x_raw:
                        x_raw[what, unit] = x_pool.tile([P, HALVES, UNIT_K], BF16, name="x%d" % what, tag="x%d" % what)
                    load_pixels(what, x_raw[what, unit], first, count)
                else:
                    if unit not in wi_raw:
                        wi_raw[unit] = wi_raw_pool.tile([P, UNIT, PACK, F_OUT], BF16, name="raw")
                    load_wi(wi_raw[unit], first, count)

        issue_loads(0)
        nc.sync.dma_start(out=bias_rows[0:F_TILES, :], in_=bi.rearrange("(f c) -> f c", f=F_TILES))
        issue_loads(AHEAD - 1)

        xi_copies = []
        for b in range(IMAGES):
            xi = const.tile([P, 3, F_TILES, XI_WIDTH], F32, name="xi%d" % b)
            nc.vector.memset(xi[:], 0.0)
            xi_copies.append(xi)

        wi_codes = const.tile([P, PASSES * F_OUT], U32, align_bytes=64)
        wi_scales = const.tile([P, PASSES * F_OUT], U8, align_bytes=64)
        result = const.tile([P, ALL_WINDOWS * WIN_OUT], F32)

        def regroup_wi(first):
            raw = wi_raw[first // UNIT]
            grouped = wi_grp_pool.tile([P, STEP, F_OUT, PACK], BF16, align_bytes=64, name="wi_grp")
            for g in range(STEP):
                dst = grouped[:, g, :, :].rearrange("p (c i) t -> p c t i", i=4)
                src = raw[:, (first + g) % UNIT, :, :].rearrange("p t (c i) -> p c t i", i=4)
                split = (F_OUT if g < STEP - 1 or first == PASSES - STEP else WI_VECTOR) // 4
                nc.vector.tensor_copy(out=dst[:, :split], in_=src[:, :split])
                if split < F_OUT // 4:
                    nc.scalar.copy(out=dst[:, split:], in_=src[:, split:])
            return grouped

        def quantise_wi(first, grouped):
            cols = slice(first * F_OUT, (first + STEP) * F_OUT)
            nc.vector.quantize_mx(
                out=wi_codes[:, cols].bitcast(FP8X4),
                scales=wi_scales[:, cols],
                in_=grouped[:].rearrange("p g c t -> p (g c t)"),
            )

        def part_words(raw, h, first, engine):
            o0 = (first % UNIT) * PASS_WORDS
            parted = part_pool.tile([P, 2, STEP * P], F32, name="parted", tag="parted")
            src = raw[:, h, :].bitcast(F32)[:, o0 : o0 + STEP * PASS_WORDS].rearrange("p (w u) -> p u w", u=2)
            if engine == "v":
                nc.vector.tensor_copy(out=parted[:], in_=src)
            else:
                nc.scalar.copy(out=parted[:], in_=src)
            return parted

        def transpose_x(raw, parted, first, tag, tags):
            grouped = grp_pool.tile([P, STEP, IMG_PIX * PACK], BF16, align_bytes=64, name=tag, tag=tag)
            for g in range(STEP):
                flipped = work_bank(tags)
                first_word = ((first + g) % UNIT) * PASS_WORDS
                for u in range(2):
                    for h in range(HALVES):
                        col = u * IMG_PIX + h * P
                        if h in parted:
                            words = parted[h][:, u, g * P : (g + 1) * P]
                        else:
                            words = raw[:, h, :].bitcast(F32)[:, first_word + u : first_word + PASS_WORDS : 2]
                        nc.tensor.transpose(flipped[:, col : col + P], words, ident[:])
                nc.scalar.copy(
                    out=grouped[:, g, :].bitcast(F32).rearrange("p (r u) -> p r u", u=2),
                    in_=flipped[:].rearrange("p (u r) -> p r u", u=2),
                )
            return grouped

        def quantise_x(grouped, tag):
            codes = mx_pool.tile([P, STEP * IMG_PIX], U32, align_bytes=64, name=tag + "c", tag=tag + "c")
            scales = mx_pool.tile([P, STEP * IMG_PIX], U8, align_bytes=64, name=tag + "s", tag=tag + "s")
            nc.vector.quantize_mx(
                out=codes[:].bitcast(FP8X4), scales=scales[:], in_=grouped[:].rearrange("p g n -> p (g n)")
            )
            return codes, scales

        def multiply(first, acc, codes, scales):
            for g in range(STEP):
                k_pass = first + g
                cols = slice(g * IMG_PIX, (g + 1) * IMG_PIX)
                for f in range(F_TILES):
                    columns = slice(k_pass * F_OUT + f * P, k_pass * F_OUT + (f + 1) * P)
                    nc.tensor.matmul_mx(
                        out=acc[f][:, 0:IMG_PIX],
                        lhsT=wi_codes[:, columns].bitcast(FP8X4),
                        lhsT_scale=wi_scales[:, columns],
                        rhs=codes[:, cols].bitcast(FP8X4),
                        rhs_scale=scales[:, cols],
                        start=(k_pass == 0),
                        stop=(k_pass == PASSES - 1),
                    )

        def spread_xi(b, acc):
            xi = xi_copies[b]
            for j in range(3):
                v_lo = max(0, j - 1)
                v_hi = min(SIDE, SIDE - 1 + j)
                first = XI_LEFT - (j - 1)
                for f in range(F_TILES):
                    image = acc[f][:, 0:IMG_PIX].rearrange("p (u v) -> p u v", v=SIDE)
                    dst = xi[:, j, f, first : first + IMG_PIX].rearrange("p (u v) -> p u v", v=SIDE)
                    if f == 0 or (b == 1 and j == 2):
                        nc.scalar.activation(
                            out=dst[:, :, v_lo:v_hi],
                            in_=image[:, :, v_lo:v_hi],
                            func=ACT.Identity,
                            bias=bias_col[:, f : f + 1],
                            scale=1.0,
                        )
                    else:
                        nc.vector.tensor_scalar(
                            out=dst[:, :, v_lo:v_hi],
                            in0=image[:, :, v_lo:v_hi],
                            scalar1=bias_col[:, f : f + 1],
                            scalar2=None,
                            op0=ALU.add,
                        )

        def weigh_window(e, products, place, tags, direct, by_tap):
            r, wd = divmod(e, WINDOWS)
            b, h = divmod(r, HALVES)
            xi = xi_copies[b]
            first_block = (WIN * wd) // P
            skip = WIN * wd - first_block * P
            patch = work_bank(tags)
            for s in range(WIN_BLOCKS):
                t, f = divmod(first_block + s, F_TILES)
                i, j = divmod(t, 3)
                start = XI_LEFT + h * P + (i - 1) * SIDE
                nc.tensor.transpose(patch[:, s * P : (s + 1) * P], xi[:, j, f, start : start + P], ident[:])
            weights = w_sb[:, r, WIN_GROUPS * TAPS * wd : WIN_GROUPS * TAPS * (wd + 1)]
            if by_tap:
                order = "p (g c m) -> p m g c"
                weights = (
                    weights.rearrange("p (g m) -> p m g", m=TAPS)
                    .unsqueeze(3)
                    .to_broadcast([P, TAPS, WIN_GROUPS, GROUP_CH])
                )
                weighed = products.rearrange("p (m o) -> p m o", m=TAPS)[:, :, WIN_OUT * place : WIN_OUT * (place + 1)]
                weighed = weighed.rearrange("p m (g c) -> p m g c", g=WIN_GROUPS)
            else:
                order = "p (g c m) -> p g c m"
                weights = (
                    weights.rearrange("p (g m) -> p g m", m=TAPS)
                    .unsqueeze(2)
                    .to_broadcast([P, WIN_GROUPS, GROUP_CH, TAPS])
                )
                weighed = products[:, WIN * place : WIN * (place + 1)].rearrange(
                    "p (g c m) -> p g c m", g=WIN_GROUPS, m=TAPS
                )
            entries = patch[:, skip : skip + WIN]
            if direct:
                nc.vector.tensor_tensor(
                    out=weighed, in0=entries.rearrange(order, g=WIN_GROUPS, m=TAPS), in1=weights, op=ALU.mult
                )
            else:
                patch_sb = patch_sb_pool.tile([P, WIN], F32)
                nc.scalar.copy(out=patch_sb[:], in_=entries)
                nc.gpsimd.tensor_tensor(
                    out=weighed, in0=patch_sb[:].rearrange(order, g=WIN_GROUPS, m=TAPS), in1=weights, op=ALU.mult
                )

        def add_nines(products, bank_tile):
            for m in range(TAPS):
                nc.tensor.matmul(
                    bank_tile[:, 0:P],
                    lhsT=products[:, m * P : (m + 1) * P],
                    rhs=ident[:],
                    is_transpose=True,
                    start=(m == 0),
                    stop=(m == TAPS - 1),
                )
            sums_sb = patch_sb_pool.tile([P, P], F32, name="sums_sb")
            nc.scalar.copy(out=sums_sb[:], in_=bank_tile[:, 0:P])
            return sums_sb

        def turn_back(first, sums_sb, bank_tile):
            nc.tensor.transpose(bank_tile[:, 0:P], sums_sb[:], ident[:])
            nc.scalar.copy(out=result[:, WIN_OUT * first : WIN_OUT * first + P], in_=bank_tile[:, 0:P])

        def sum_windows(first, count, products):
            nc.vector.tensor_reduce(
                out=result[:, WIN_OUT * first : WIN_OUT * (first + count)],
                in_=products[:, 0 : WIN * count].rearrange("p (o m) -> p o m", m=TAPS),
                axis=AXIS.X,
                op=ALU.add,
            )

        def store(r, lo, hi):
            nc.sync.dma_start(
                out=out_rows[r * P : (r + 1) * P, lo:hi], in_=result[:, r * F_OUT + lo : r * F_OUT + hi]
            )

        acc = [[bank("acc%d%d" % (b, f)) for f in range(F_TILES)] for b in range(IMAGES)]
        grouped = {}
        wi_grouped = {}
        mx = {}

        def step_images(n):
            return [(b, m) for b, m in enumerate(turn_steps[n]) if m is not None] if n < turns else []

        def transpose_step(n):
            tags = WORK_A if n < STEPS + TLEAD else WORK_B
            for b, m in step_images(n):
                grouped[b, m] = transpose_x(x_raw[b, m * STEP // UNIT], parted.get((b, m), {}), m * STEP, "x%dg" % b, tags)

        def regroup_step(n):
            if n < STEPS:
                wi_grouped[n] = regroup_wi(n * STEP)

        parted = {}

        def part_step(n):
            for b, m in step_images(n):
                who = PARTING[b] if n < STEPS else PARTING_LATE
                if n < PART_FROM:
                    who = []
                parted[b, m] = {h: part_words(x_raw[b, m * STEP // UNIT], h, m * STEP, e) for h, e in who}

        def quantise_step(n, image):
            for b, m in step_images(n):
                if b == image:
                    mx[b, m] = quantise_x(grouped[b, m], "x%d" % b)

        def quantise_wi_step(n):
            if n < STEPS:
                quantise_wi(n * STEP, wi_grouped[n])

        def weigh_windows(first, tags):
            group = first // TURN_WINDOWS
            gps = GPS_OF.get(group, GPS)
            products = products_pool.tile([P, TURN_WINDOWS * WIN], F32, name="products")
            for i in range(TURN_WINDOWS):
                weigh_window(first + i, products[:], i, tags, i not in gps, group == TENSOR_SUM)
            return first, products

        def store_windows(first):
            r, wd = divmod(first, WINDOWS)
            store(r, WIN_OUT * wd, WIN_OUT * (wd + TURN_WINDOWS))

        def finish_windows(first, products):
            sum_windows(first, TURN_WINDOWS, products)
            store_windows(first)

        for n in range(PLEAD - TLEAD):
            part_step(n)
        for n in range(TLEAD):
            transpose_step(n)
            if n == 0:
                transpose_bias()
            part_step(n + PLEAD - TLEAD)
            if n < QLEAD:
                for b in range(IMAGES):
                    quantise_step(n, b)
        for n in range(RLEAD):
            regroup_step(n)
            if n < WLEAD:
                quantise_wi_step(n)
        waiting = None
        done = 0
        for n in range(turns):
            issue_loads(n + AHEAD)
            if n == turns + WI_LAG - 1 - AHEAD:
                load_weights()
            quantise_step(n + QLEAD, 0)
            quantise_wi_step(n + WLEAD)
            quantise_step(n + QLEAD, 1)
            transpose_step(n + TLEAD)
            regroup_step(n + RLEAD)
            part_step(n + PLEAD)
            for b, m in step_images(n):
                multiply(m * STEP, acc[b], mx[b, m][0], mx[b, m][1])
            if n == STEPS - 1:
                spread_xi(0, acc[0])
            if n == turns - 1:
                spread_xi(1, acc[1])
            if n >= STEPS and done < HALVES * WINDOWS:
                following = weigh_windows(done, WORK_B)
                if waiting:
                    finish_windows(waiting[0], waiting[1])
                waiting = following
                done += TURN_WINDOWS
        for_tensor = None
        for first in range(done, ALL_WINDOWS, TURN_WINDOWS):
            following = weigh_windows(first, WORK_C)
            if waiting[0] // TURN_WINDOWS == TENSOR_SUM:
                for_tensor = waiting
            else:
                finish_windows(waiting[0], waiting[1])
            waiting = following
        sums_sb = add_nines(for_tensor[1][:], work_bank(WORK_C))
        turn_back(for_tensor[0], sums_sb, work_bank(WORK_C))
        store_windows(for_tensor[0])
        finish_windows(waiting[0], waiting[1])
